import numpy as np
import ml_dtypes


def mxq(x, axis, fmt="e4m3"):
    dtype, down = {"e4m3": (ml_dtypes.float8_e4m3fn, 7), "e5m2": (ml_dtypes.float8_e5m2, 14)}[fmt]
    v = np.moveaxis(np.asarray(x, np.float32).astype(ml_dtypes.bfloat16).astype(np.float64), axis, -1)
    blocks = v.reshape(v.shape[:-1] + (-1, 32))
    amax = np.abs(blocks).max(-1, keepdims=True)
    byte = np.maximum(np.where(amax > 0, np.frexp(amax)[1] - 1 + 127, 0) - down, 1)
    scale = np.exp2(byte - 127.0)
    codes = (blocks / scale).astype(np.float32).astype(dtype).astype(np.float64)
    return np.moveaxis((codes * scale).reshape(v.shape), -1, axis)


WIDE = False


def mx_kscale(k):
    if not WIDE:
        return np.ones(k)
    levels = np.array([10, -10, 5, -5, 0])
    a = np.random.permutation(np.resize(levels, k // 512 * 4)).reshape(k // 512, 4)
    idx = np.arange(k)
    return np.exp2(a[idx // 512, idx % 128 // 32])


BF16 = ml_dtypes.bfloat16


def bf(x):
    return np.asarray(x, np.float32).astype(BF16)


def f64(x):
    return np.asarray(x).astype(np.float64)


B, IN, HID, PROJ, H, KC = 128, 2048, 2048, 2048, 4, 4
BH = HID // H
BI = PROJ // H


def sigmoid(v):
    return 1.0 / (1.0 + np.exp(-v))


def silu(v):
    return v / (1.0 + np.exp(-v))


def blockdiag(vq, w, b):
    y = vq.reshape(B, H, BI).transpose(1, 0, 2) @ mxq(f64(w), 1, "e4m3")
    return y.transpose(1, 0, 2).reshape(B, HID) + f64(b)


def setup_inputs():
    s, t = mx_kscale(PROJ), mx_kscale(PROJ)
    sh, th = s.reshape(H, BI, 1), t.reshape(H, BI, 1)
    r = np.random.standard_normal
    return {"x_conv": bf(silu(r((B, PROJ))) * s), "x_left": bf(r((B, PROJ)) * t),
            "c_prev": bf(r((B, HID))), "n_prev": bf(r((B, HID))), "m_prev": bf(0.5 * r((B, HID))),
            "wq_w": bf(r((H, BI, BH)) * 1.5 / np.sqrt(BI) / sh), "wq_b": bf(0.2 * r(HID)),
            "wk_w": bf(r((H, BI, BH)) * 0.5 * np.sqrt(BH) / np.sqrt(BI) / sh), "wk_b": bf(0.1 * np.sqrt(BH) * r(HID)),
            "wv_w": bf(r((H, BI, BH)) / np.sqrt(BI) / th), "wv_b": bf(0.2 * r(HID)),
            "wi_w": bf(r((PROJ, HID)) * 1.5 / np.sqrt(PROJ) / s[:, None]), "wi_b": bf(0.2 * r(HID)),
            "wf_w": bf(r((PROJ, HID)) * 1.5 / np.sqrt(PROJ) / s[:, None]), "wf_b": bf(0.2 * r(HID)),
            "wo_w": bf(r((PROJ, HID)) / np.sqrt(PROJ) / t[:, None]), "wo_b": bf(0.2 * r(HID))}


def reference(x_conv, x_left, c_prev, n_prev, m_prev, wq_w, wq_b, wk_w, wk_b, wv_w, wv_b, wi_w, wi_b, wf_w, wf_b, wo_w, wo_b):
    xc = mxq(f64(x_conv), 1, "e4m3")
    xl = mxq(f64(x_left), 1, "e4m3")
    q = blockdiag(xc, wq_w, wq_b)
    k = blockdiag(xc, wk_w, wk_b) / np.sqrt(BH)
    v = blockdiag(xl, wv_w, wv_b)
    i_tilde = (xc @ mxq(f64(wi_w), 0, "e4m3")) + f64(wi_b)
    f_tilde = (xc @ mxq(f64(wf_w), 0, "e4m3")) + f64(wf_b)
    o = sigmoid((xl @ mxq(f64(wo_w), 0, "e4m3")) + f64(wo_b))
    m_t = np.maximum(f_tilde + f64(m_prev), i_tilde)
    i = np.exp(i_tilde - m_t)
    f = np.exp(f_tilde + f64(m_prev) - m_t)
    c_t = f * f64(c_prev) + i * (v * k)
    n_t = f * f64(n_prev) + i * k
    denom = np.sqrt(np.sum((n_t * q) ** 2, axis=-1, keepdims=True)) + 1e-6
    h_t = o * (c_t * q) / denom
    return h_t, c_t, n_t, m_t

@@ -1,0 +1,274 @@
+from contextlib import ExitStack
+import math
+
+import concourse.mybir as mybir
+from concourse.masks import make_identity
+
+BF16 = mybir.dt.bfloat16
+F32 = mybir.dt.float32
+U32 = mybir.dt.uint32
+U8 = mybir.dt.uint8
+FP8X4 = mybir.dt.float8_e4m3fn_x4
+ALU = mybir.AluOpType
+ACT = mybir.ActivationFunctionType
+
+P = 128
+PACK = 4
+K_PASS = P * PACK
+WIDTH = 2048
+QUARTER = 512
+QUARTERS = WIDTH // QUARTER
+K_PASSES = WIDTH // K_PASS
+
+RING = 6
+PIECES_AHEAD = 6
+PSUM_BANKS = 8
+
+K_SCALE = 1.0 / math.sqrt(QUARTER)
+EPSILON = 1e-6
+
+FLOPS = 2 * P * (3 * WIDTH * WIDTH + 3 * QUARTERS * QUARTER * QUARTER)
+
+
+def columns(quarter):
+    return slice(quarter * QUARTER, (quarter + 1) * QUARTER)
+
+
+def tile_mlstmblock_pb_kernel(
+    tc,
+    x_conv, x_left, c_prev, n_prev, m_prev,
+    wq_w, wq_b, wk_w, wk_b, wv_w, wv_b, wi_w, wi_b, wf_w, wf_b, wo_w, wo_b,
+    out_0, out_1, out_2, out_3,
+):
+    nc = tc.nc
+    with ExitStack() as ctx:
+        keep = ctx.enter_context(tc.tile_pool(name="keep", bufs=1))
+        ring = ctx.enter_context(tc.tile_pool(name="ring", bufs=RING))
+        work = ctx.enter_context(tc.tile_pool(name="work", bufs=PIECES_AHEAD))
+        psum = ctx.enter_context(tc.psum_pool(name="psum", bufs=PSUM_BANKS))
+
+        def load_rows(sources):
+            pack = ring.tile([P, PACK, WIDTH], BF16, name="pack", tag="ring")
+            for slot, source in enumerate(sources):
+                nc.sync.dma_start(out=pack[:, slot, :], in_=source)
+            return pack
+
+        def load_dense(weights, k_pass):
+            raw = ring.tile([P, PACK, WIDTH], BF16, name="raw", tag="ring")
+            rows = weights[k_pass * K_PASS : (k_pass + 1) * K_PASS, :]
+            nc.sync.dma_start(out=raw[:], in_=rows.rearrange("(p j) n -> p j n", j=PACK))
+            return [raw[:, :, columns(quarter)] for quarter in range(QUARTERS)]
+
+        def load_heads(weights):
+            raw = ring.tile([P, QUARTERS, PACK * QUARTER], BF16, name="raw", tag="ring")
+            nc.sync.dma_start(out=raw[:], in_=weights.rearrange("h (p j) o -> p h (j o)", j=PACK))
+            return [
+                raw[:, head, :].rearrange("p (j o) -> p j o", j=PACK) for head in range(QUARTERS)
+            ]
+
+        identity = keep.tile([P, P], F32)
+        make_identity(nc, identity[:])
+
+        def quantise_activations(x_rows, name):
+            words = x_rows.bitcast(F32).rearrange("b (c p u) -> b c u p", p=P, u=2)
+            grouped = work.tile([P, WIDTH], BF16, align_bytes=64, name="x_grouped", bufs=1)
+            grouped_words = grouped[:].bitcast(F32).rearrange("p (c b u) -> p c b u", b=P, u=2)
+            for half in range(2):
+                turned = psum.tile([P, 2, 2, P], F32, name="turned", tag="bank")
+                for c in range(2):
+                    for u in range(2):
+                        nc.tensor.transpose(
+                            turned[:, c, u, :], words[:, 2 * half + c, u, :], identity[:]
+                        )
+                copy_out = nc.vector.tensor_copy if half == 0 else nc.scalar.copy
+                copy_out(
+                    out=grouped_words[:, 2 * half : 2 * half + 2, :, :],
+                    in_=turned[:].rearrange("p c u b -> p c b u"),
+                )
+            codes = keep.tile([P, K_PASSES * P], U32, align_bytes=64, name=name + "_codes")
+            scales = keep.tile([P, K_PASSES * P], U8, align_bytes=64, name=name + "_scales")
+            nc.vector.quantize_mx(out=codes[:].bitcast(FP8X4), scales=scales[:], in_=grouped[:])
+            return codes, scales
+
+        def multiply_piece(piece, on_vector, x, k_pass, bank, start, stop):
+            grouped = work.tile([P, QUARTER, PACK], BF16, align_bytes=64, name="grouped")
+            copy = nc.vector.tensor_copy if on_vector else nc.scalar.copy
+            copy(
+                out=grouped[:].rearrange("p (c i) j -> p c j i", i=4),
+                in_=piece.rearrange("p j (c i) -> p c j i", i=4),
+            )
+            codes = work.tile([P, QUARTER], U32, align_bytes=64, name="codes")
+            scales = work.tile([P, QUARTER], U8, align_bytes=64, name="scales")
+            nc.vector.quantize_mx(
+                out=codes[:].bitcast(FP8X4),
+                scales=scales[:],
+                in_=grouped[:].rearrange("p w j -> p (w j)"),
+            )
+            x_codes, x_scales = x
+            batch = slice(k_pass * P, (k_pass + 1) * P)
+            nc.tensor.matmul_mx(
+                out=bank[:],
+                lhsT=x_codes[:, batch].bitcast(FP8X4),
+                lhsT_scale=x_scales[:, batch],
+                rhs=codes[:].bitcast(FP8X4),
+                rhs_scale=scales[:],
+                start=start,
+                stop=stop,
+            )
+
+        def regroups_on_vector(quarter, carried):
+            return carried is None and quarter % 2 == 0
+
+        def multiply_dense(weights, x, carried):
+            banks = []
+            for k_pass in range(K_PASSES):
+                pieces = load_dense(weights, k_pass)
+                for quarter in range(QUARTERS):
+                    if carried is not None:
+                        carried(quarter)
+                    if k_pass == 0:
+                        banks.append(psum.tile([P, QUARTER], F32, name="bank", tag="bank"))
+                    multiply_piece(
+                        pieces[quarter], regroups_on_vector(quarter, carried), x, k_pass,
+                        banks[quarter], start=(k_pass == 0), stop=(k_pass == K_PASSES - 1),
+                    )
+                carried = None
+            return banks
+
+        def multiply_heads(pieces, x, carried):
+            banks = []
+            for head in range(QUARTERS):
+                carried(head)
+                banks.append(psum.tile([P, QUARTER], F32, name="bank", tag="bank"))
+                multiply_piece(
+                    pieces[head], regroups_on_vector(head, carried), x, head,
+                    banks[head], start=True, stop=True,
+                )
+            return banks
+
+        i_gate = keep.tile([P, WIDTH], F32)
+        f_gate = keep.tile([P, WIDTH], F32)
+        m_t = keep.tile([P, WIDTH], F32)
+        n_t = keep.tile([P, WIDTH], F32)
+        c_t = keep.tile([P, WIDTH], F32)
+        ik = keep.tile([P, WIDTH], F32)
+        ikv = keep.tile([P, WIDTH], F32)
+        q = keep.tile([P, WIDTH], F32)
+        nq = keep.tile([P, WIDTH], F32)
+        h_t = keep.tile([P, WIDTH], F32)
+        squares = keep.tile([P, QUARTERS], F32)
+        denom = keep.tile([P, 1], F32)
+        denom_inverse = keep.tile([P, 1], F32)
+
+        xc = quantise_activations(load_rows([x_conv])[:, 0, :], "xc")
+        banks_i = multiply_dense(wi_w, xc, None)
+        banks_f = multiply_dense(wf_w, xc, None)
+
+        pieces_k = load_heads(wk_w)
+        gate_rows = load_rows(
+            [wi_b.partition_broadcast(P), wf_b.partition_broadcast(P), m_prev, n_prev]
+        )
+        bias_i, bias_f, m_old, n_old = [gate_rows[:, slot, :] for slot in range(4)]
+        cell_rows = load_rows(
+            [c_prev, wk_b.partition_broadcast(P), x_left, wv_b.partition_broadcast(P)]
+        )
+        c_old, bias_k, x_left_rows, bias_v = [cell_rows[:, slot, :] for slot in range(4)]
+
+        nc.vector.tensor_tensor(out=f_gate[:], in0=bias_f, in1=m_old, op=ALU.add)
+
+        def finish_gates(quarter):
+            cols = columns(quarter)
+            nc.vector.tensor_tensor(
+                out=i_gate[:, cols], in0=banks_i[quarter][:], in1=bias_i[:, cols], op=ALU.add
+            )
+            nc.vector.tensor_tensor(
+                out=f_gate[:, cols], in0=banks_f[quarter][:], in1=f_gate[:, cols], op=ALU.add
+            )
+            nc.vector.tensor_tensor(
+                out=m_t[:, cols], in0=i_gate[:, cols], in1=f_gate[:, cols], op=ALU.max
+            )
+            nc.gpsimd.dma_start(out=out_3[:, cols], in_=m_t[:, cols])
+            for gate in (i_gate, f_gate):
+                nc.vector.tensor_tensor(
+                    out=gate[:, cols], in0=gate[:, cols], in1=m_t[:, cols], op=ALU.subtract
+                )
+                nc.scalar.activation(out=gate[:, cols], in_=gate[:, cols], func=ACT.Exp)
+            nc.vector.tensor_tensor(
+                out=n_t[:, cols], in0=f_gate[:, cols], in1=n_old[:, cols], op=ALU.mult
+            )
+            nc.vector.tensor_tensor(
+                out=c_t[:, cols], in0=f_gate[:, cols], in1=c_old[:, cols], op=ALU.mult
+            )
+
+        banks_k = multiply_heads(pieces_k, xc, finish_gates)
+
+        def finish_k(quarter):
+            cols = columns(quarter)
+            nc.vector.tensor_tensor(
+                out=ik[:, cols], in0=banks_k[quarter][:], in1=bias_k[:, cols], op=ALU.add
+            )
+            nc.vector.tensor_tensor(
+                out=ik[:, cols], in0=ik[:, cols], in1=i_gate[:, cols], op=ALU.mult
+            )
+            nc.vector.scalar_tensor_tensor(
+                out=n_t[:, cols], in0=ik[:, cols], scalar=K_SCALE, in1=n_t[:, cols],
+                op0=ALU.mult, op1=ALU.add,
+            )
+            nc.gpsimd.dma_start(out=out_2[:, cols], in_=n_t[:, cols])
+
+        pieces_v = load_heads(wv_w)
+        xl = quantise_activations(x_left_rows, "xl")
+        banks_v = multiply_heads(pieces_v, xl, finish_k)
+
+        def finish_v(quarter):
+            cols = columns(quarter)
+            nc.vector.tensor_tensor(
+                out=ikv[:, cols], in0=banks_v[quarter][:], in1=bias_v[:, cols], op=ALU.add
+            )
+            nc.vector.tensor_tensor(
+                out=ikv[:, cols], in0=ikv[:, cols], in1=ik[:, cols], op=ALU.mult
+            )
+            nc.vector.scalar_tensor_tensor(
+                out=c_t[:, cols], in0=ikv[:, cols], scalar=K_SCALE, in1=c_t[:, cols],
+                op0=ALU.mult, op1=ALU.add,
+            )
+            nc.gpsimd.dma_start(out=out_1[:, cols], in_=c_t[:, cols])
+
+        pieces_q = load_heads(wq_w)
+        last_rows = load_rows([wq_b.partition_broadcast(P), wo_b.partition_broadcast(P)])
+        bias_q, bias_o = [last_rows[:, slot, :] for slot in range(2)]
+        banks_q = multiply_heads(pieces_q, xc, finish_v)
+
+        def finish_q(quarter):
+            cols = columns(quarter)
+            nc.vector.tensor_tensor(
+                out=q[:, cols], in0=banks_q[quarter][:], in1=bias_q[:, cols], op=ALU.add
+            )
+            nc.vector.tensor_tensor(
+                out=nq[:, cols], in0=n_t[:, cols], in1=q[:, cols], op=ALU.mult
+            )
+            nc.scalar.activation(
+                out=nq[:, cols], in_=nq[:, cols], func=ACT.Square,
+                accum_out=squares[:, quarter : quarter + 1],
+            )
+            if quarter == QUARTERS - 1:
+                nc.vector.reduce_sum(out=denom[:], in_=squares[:], axis=mybir.AxisListType.X)
+                nc.scalar.sqrt(out=denom[:], in_=denom[:])
+                nc.vector.tensor_scalar_add(out=denom[:], in0=denom[:], scalar1=EPSILON)
+                nc.vector.reciprocal(out=denom_inverse[:], in_=denom[:])
+                nc.vector.scalar_tensor_tensor(
+                    out=q[:], in0=c_t[:], scalar=denom_inverse[:, 0:1], in1=q[:],
+                    op0=ALU.mult, op1=ALU.mult,
+                )
+
+        banks_o = multiply_dense(wo_w, xl, finish_q)
+        for quarter in range(QUARTERS):
+            cols = columns(quarter)
+            nc.vector.tensor_tensor(
+                out=h_t[:, cols], in0=banks_o[quarter][:], in1=bias_o[:, cols], op=ALU.add
+            )
+            nc.scalar.activation(out=h_t[:, cols], in_=h_t[:, cols], func=ACT.Sigmoid)
+            nc.vector.tensor_tensor(
+                out=h_t[:, cols], in0=h_t[:, cols], in1=q[:, cols], op=ALU.mult
+            )
+            nc.sync.dma_start(out=out_0[:, cols], in_=h_t[:, cols])

@@ -59,6 +59,20 @@ def tile_mlstmblock_pb_kernel(
             nc.sync.dma_start(out=raw[:], in_=rows.rearrange("(p j) n -> p j n", j=PACK))
             return [raw[:, :, columns(quarter)] for quarter in range(QUARTERS)]
 
+        def load_dense_piecewise(weights, k_pass):
+            raw = ring.tile([P, QUARTERS, PACK * QUARTER], BF16, name="raw", tag="ring")
+            rows = weights[k_pass * K_PASS : (k_pass + 1) * K_PASS, :]
+            pieces = [
+                raw[:, quarter, :].rearrange("p (j n) -> p j n", j=PACK)
+                for quarter in range(QUARTERS)
+            ]
+            for quarter in range(QUARTERS):
+                nc.sync.dma_start(
+                    out=pieces[quarter],
+                    in_=rows[:, columns(quarter)].rearrange("(p j) n -> p j n", j=PACK),
+                )
+            return pieces
+
         def load_heads(weights):
             raw = ring.tile([P, QUARTERS, PACK * QUARTER], BF16, name="raw", tag="ring")
             nc.sync.dma_start(out=raw[:], in_=weights.rearrange("h (p j) o -> p h (j o)", j=PACK))
@@ -116,22 +130,26 @@ def tile_mlstmblock_pb_kernel(
                 stop=stop,
             )
 
-        def regroups_on_vector(quarter, carried):
-            return carried is None and quarter % 2 == 0
-
-        def multiply_dense(weights, x, carried):
+        def multiply_dense(
+            weights, x, carried=None, after_first_chunk=None, piecewise_start=False
+        ):
             banks = []
             for k_pass in range(K_PASSES):
-                pieces = load_dense(weights, k_pass)
+                if piecewise_start and k_pass == 0:
+                    pieces = load_dense_piecewise(weights, k_pass)
+                else:
+                    pieces = load_dense(weights, k_pass)
                 for quarter in range(QUARTERS):
                     if carried is not None:
                         carried(quarter)
                     if k_pass == 0:
                         banks.append(psum.tile([P, QUARTER], F32, name="bank", tag="bank"))
                     multiply_piece(
-                        pieces[quarter], regroups_on_vector(quarter, carried), x, k_pass,
+                        pieces[quarter], carried is None and quarter % 2 == 0, x, k_pass,
                         banks[quarter], start=(k_pass == 0), stop=(k_pass == K_PASSES - 1),
                     )
+                if k_pass == 0 and after_first_chunk is not None:
+                    after_first_chunk()
                 carried = None
             return banks
 
@@ -141,7 +159,7 @@ def tile_mlstmblock_pb_kernel(
                 carried(head)
                 banks.append(psum.tile([P, QUARTER], F32, name="bank", tag="bank"))
                 multiply_piece(
-                    pieces[head], regroups_on_vector(head, carried), x, head,
+                    pieces[head], False, x, head,
                     banks[head], start=True, stop=True,
                 )
             return banks
@@ -157,12 +175,14 @@ def tile_mlstmblock_pb_kernel(
         nq = keep.tile([P, WIDTH], F32)
         h_t = keep.tile([P, WIDTH], F32)
         squares = keep.tile([P, QUARTERS], F32)
-        denom = keep.tile([P, 1], F32)
-        denom_inverse = keep.tile([P, 1], F32)
+        norm = keep.tile([P, 1], F32)
+        half_over_denom = keep.tile([P, 1], F32)
+        one_half = keep.tile([P, 1], F32)
+        nc.vector.memset(one_half[:], 0.5)
 
         xc = quantise_activations(load_rows([x_conv])[:, 0, :], "xc")
-        banks_i = multiply_dense(wi_w, xc, None)
-        banks_f = multiply_dense(wf_w, xc, None)
+        banks_i = multiply_dense(wi_w, xc, piecewise_start=True)
+        banks_f = multiply_dense(wf_w, xc)
 
         pieces_k = load_heads(wk_w)
         gate_rows = load_rows(
@@ -251,24 +271,33 @@ def tile_mlstmblock_pb_kernel(
                 out=nq[:, cols], in_=nq[:, cols], func=ACT.Square,
                 accum_out=squares[:, quarter : quarter + 1],
             )
-            if quarter == QUARTERS - 1:
-                nc.vector.reduce_sum(out=denom[:], in_=squares[:], axis=mybir.AxisListType.X)
-                nc.scalar.sqrt(out=denom[:], in_=denom[:])
-                nc.vector.tensor_scalar_add(out=denom[:], in0=denom[:], scalar1=EPSILON)
-                nc.vector.reciprocal(out=denom_inverse[:], in_=denom[:])
+
+        def normalise():
+            nc.vector.reduce_sum(out=norm[:], in_=squares[:], axis=mybir.AxisListType.X)
+            nc.gpsimd.tensor_tensor(out=norm[:], in0=norm[:], in1=one_half[:], op=ALU.pow)
+            nc.vector.tensor_scalar(
+                out=norm[:], in0=norm[:], scalar1=2.0, scalar2=2.0 * EPSILON,
+                op0=ALU.mult, op1=ALU.add,
+            )
+            nc.vector.reciprocal(out=half_over_denom[:], in_=norm[:])
+            for quarter in range(QUARTERS):
+                cols = columns(quarter)
                 nc.vector.scalar_tensor_tensor(
-                    out=q[:], in0=c_t[:], scalar=denom_inverse[:, 0:1], in1=q[:],
-                    op0=ALU.mult, op1=ALU.mult,
+                    out=q[:, cols], in0=c_t[:, cols], scalar=half_over_denom[:, 0:1],
+                    in1=q[:, cols], op0=ALU.mult, op1=ALU.mult,
                 )
 
-        banks_o = multiply_dense(wo_w, xl, finish_q)
+        banks_o = multiply_dense(
+            wo_w, xl, carried=finish_q, after_first_chunk=normalise
+        )
         for quarter in range(QUARTERS):
             cols = columns(quarter)
             nc.vector.tensor_tensor(
                 out=h_t[:, cols], in0=banks_o[quarter][:], in1=bias_o[:, cols], op=ALU.add
             )
-            nc.scalar.activation(out=h_t[:, cols], in_=h_t[:, cols], func=ACT.Sigmoid)
-            nc.vector.tensor_tensor(
-                out=h_t[:, cols], in0=h_t[:, cols], in1=q[:, cols], op=ALU.mult
+            nc.scalar.activation(out=h_t[:, cols], in_=h_t[:, cols], func=ACT.Tanh, scale=0.5)
+            nc.vector.scalar_tensor_tensor(
+                out=h_t[:, cols], in0=h_t[:, cols], scalar=1.0, in1=q[:, cols],
+                op0=ALU.add, op1=ALU.mult,
             )
             nc.sync.dma_start(out=out_0[:, cols], in_=h_t[:, cols])

@@ -18,10 +18,12 @@ K_PASS = P * PACK
 WIDTH = 2048
 QUARTER = 512
 QUARTERS = WIDTH // QUARTER
+HALF = 2 * QUARTER
 K_PASSES = WIDTH // K_PASS
+BIAS_ROWS = WIDTH // P
 
-RING = 6
-PIECES_AHEAD = 6
+RING = 9
+LEAD = 2
 PSUM_BANKS = 8
 
 K_SCALE = 1.0 / math.sqrt(QUARTER)
@@ -41,50 +43,107 @@ def tile_mlstmblock_pb_kernel(
     out_0, out_1, out_2, out_3,
 ):
     nc = tc.nc
+    weights = {"k": wk_w, "v": wv_w, "q": wq_w, "i": wi_w, "f": wf_w, "o": wo_w}
+    bias_order = {"k": wk_b, "v": wv_b, "q": wq_b, "f": wf_b, "i": wi_b, "o": wo_b}
+
     with ExitStack() as ctx:
         keep = ctx.enter_context(tc.tile_pool(name="keep", bufs=1))
         ring = ctx.enter_context(tc.tile_pool(name="ring", bufs=RING))
-        work = ctx.enter_context(tc.tile_pool(name="work", bufs=PIECES_AHEAD))
+        work = ctx.enter_context(tc.tile_pool(name="work", bufs=4))
         psum = ctx.enter_context(tc.psum_pool(name="psum", bufs=PSUM_BANKS))
 
-        def load_rows(sources):
-            pack = ring.tile([P, PACK, WIDTH], BF16, name="pack", tag="ring")
-            for slot, source in enumerate(sources):
-                nc.sync.dma_start(out=pack[:, slot, :], in_=source)
-            return pack
-
-        def load_dense(weights, k_pass):
-            raw = ring.tile([P, PACK, WIDTH], BF16, name="raw", tag="ring")
-            rows = weights[k_pass * K_PASS : (k_pass + 1) * K_PASS, :]
-            nc.sync.dma_start(out=raw[:], in_=rows.rearrange("(p j) n -> p j n", j=PACK))
-            return [raw[:, :, columns(quarter)] for quarter in range(QUARTERS)]
-
-        def load_dense_piecewise(weights, k_pass):
-            raw = ring.tile([P, QUARTERS, PACK * QUARTER], BF16, name="raw", tag="ring")
-            rows = weights[k_pass * K_PASS : (k_pass + 1) * K_PASS, :]
-            pieces = [
-                raw[:, quarter, :].rearrange("p (j n) -> p j n", j=PACK)
-                for quarter in range(QUARTERS)
-            ]
-            for quarter in range(QUARTERS):
-                nc.sync.dma_start(
-                    out=pieces[quarter],
-                    in_=rows[:, columns(quarter)].rearrange("(p j) n -> p j n", j=PACK),
-                )
-            return pieces
-
-        def load_heads(weights):
-            raw = ring.tile([P, QUARTERS, PACK * QUARTER], BF16, name="raw", tag="ring")
-            nc.sync.dma_start(out=raw[:], in_=weights.rearrange("h (p j) o -> p h (j o)", j=PACK))
-            return [
-                raw[:, head, :].rearrange("p (j o) -> p j o", j=PACK) for head in range(QUARTERS)
-            ]
-
-        identity = keep.tile([P, P], F32)
+        identity = keep.tile([P, P], F32, name="identity")
         make_identity(nc, identity[:])
+        ctx.enter_context(tc.manual_schedule())
 
-        def quantise_activations(x_rows, name):
-            words = x_rows.bitcast(F32).rearrange("b (c p u) -> b c u p", p=P, u=2)
+        stages = []
+        stages.append([(m, head, head) for m in ("k", "v", "q") for head in range(QUARTERS)])
+        for half in range(2):
+            for m in ("i", "f"):
+                stages.append(
+                    [(m, k, 2 * half + s) for k in range(K_PASSES) for s in range(2)]
+                )
+        stages.append([("o", k, s) for k in range(K_PASSES) for s in range(2)])
+        stages.append([("o", k, 2 + s) for s in range(2) for k in range(K_PASSES)])
+        on_vector_counts = [6, 3, 4, 2, 2, 2, 2]
+        pieces = []
+        for index, stage in enumerate(stages):
+            for t, piece in enumerate(stage):
+                share = on_vector_counts[index]
+                on_vector = (t + 1) * share // len(stage) > t * share // len(stage)
+                pieces.append((piece, on_vector, index, t))
+
+        def chunk_of(piece):
+            matrix, k_pass, quarter = piece
+            return (matrix, quarter // 2) if matrix in "kvq" else (matrix, k_pass, quarter // 2)
+
+        chunk_order = []
+        for piece, other_on, other_index, other_t in pieces:
+            if chunk_of(piece) not in chunk_order:
+                chunk_order.append(chunk_of(piece))
+        last_use = {chunk_of(entry[0]): n for n, entry in enumerate(pieces)}
+
+        raw_pieces = {}
+        loaded = []
+
+        def load_next_chunk():
+            if len(loaded) == len(chunk_order):
+                return
+            chunk = chunk_order[len(loaded)]
+            loaded.append(chunk)
+            source = weights[chunk[0]]
+            if len(chunk) == 2:
+                raw = ring.tile([P, 2, PACK * QUARTER], BF16, name="raw_heads", tag="ring")
+                for s in range(2):
+                    head = 2 * chunk[1] + s
+                    nc.sync.dma_start(
+                        out=raw[:, s, :],
+                        in_=source.rearrange("h (p j) o -> p h (j o)", j=PACK)[:, head, :],
+                    )
+                    raw_pieces[(chunk[0], head, head)] = raw[:, s, :].rearrange(
+                        "p (j o) -> p j o", j=PACK
+                    )
+            else:
+                matrix, k_pass, half = chunk
+                raw = ring.tile([P, PACK, HALF], BF16, name="raw_dense", tag="ring")
+                rows = source[
+                    k_pass * K_PASS : (k_pass + 1) * K_PASS, half * HALF : (half + 1) * HALF
+                ]
+                nc.sync.dma_start(out=raw[:], in_=rows.rearrange("(p j) n -> p j n", j=PACK))
+                for s in range(2):
+                    raw_pieces[(matrix, k_pass, 2 * half + s)] = raw[:, :, columns(s)]
+
+        one_half = keep.tile([P, 1], F32, name="one_half")
+        warm = keep.tile([P, 1], F32, name="warm")
+        nc.vector.memset(one_half[:], 0.5)
+        nc.scalar.activation(out=warm[:], in_=one_half[:], func=ACT.Exp)
+
+        x_conv_rows = keep.tile([P, WIDTH], BF16, name="x_conv_rows")
+        x_left_rows = keep.tile([P, WIDTH], BF16, name="x_left_rows")
+        m_old = keep.tile([P, WIDTH], BF16, name="m_old")
+        nc_old = keep.tile([P, 2, WIDTH], BF16, name="nc_old")
+        bias_rows = keep.tile([P, P], BF16, name="bias_rows")
+        nc.gpsimd.memset(bias_rows[96:P, :], 0.0)
+        for r, matrix in enumerate(bias_order):
+            nc.gpsimd.dma_start(
+                out=bias_rows[r * BIAS_ROWS : (r + 1) * BIAS_ROWS, :],
+                in_=bias_order[matrix].rearrange("(c n) -> c n", n=P),
+            )
+        nc.sync.dma_start(out=x_conv_rows[:], in_=x_conv)
+        load_next_chunk()
+        load_next_chunk()
+        nc.sync.dma_start(out=x_left_rows[:], in_=x_left)
+        for other_more in range(RING - 2):
+            load_next_chunk()
+        nc.sync.dma_start(out=m_old[:], in_=m_prev)
+        nc.sync.dma_start(out=nc_old[:, 0, :], in_=n_prev)
+        nc.sync.dma_start(out=nc_old[:, 1, :], in_=c_prev)
+
+        identity_bf16 = keep.tile([P, P], BF16, name="identity_bf16")
+        nc.vector.tensor_copy(out=identity_bf16[:], in_=identity[:])
+
+        def turn_activations(x_rows, copy_out):
+            words = x_rows[:].bitcast(F32).rearrange("b (c p u) -> b c u p", p=P, u=2)
             grouped = work.tile([P, WIDTH], BF16, align_bytes=64, name="x_grouped", bufs=1)
             grouped_words = grouped[:].bitcast(F32).rearrange("p (c b u) -> p c b u", b=P, u=2)
             for half in range(2):
@@ -94,210 +153,311 @@ def tile_mlstmblock_pb_kernel(
                         nc.tensor.transpose(
                             turned[:, c, u, :], words[:, 2 * half + c, u, :], identity[:]
                         )
-                copy_out = nc.vector.tensor_copy if half == 0 else nc.scalar.copy
                 copy_out(
                     out=grouped_words[:, 2 * half : 2 * half + 2, :, :],
                     in_=turned[:].rearrange("p c u b -> p c b u"),
                 )
+            return grouped
+
+        def quantise_activations(grouped, name):
             codes = keep.tile([P, K_PASSES * P], U32, align_bytes=64, name=name + "_codes")
             scales = keep.tile([P, K_PASSES * P], U8, align_bytes=64, name=name + "_scales")
             nc.vector.quantize_mx(out=codes[:].bitcast(FP8X4), scales=scales[:], in_=grouped[:])
             return codes, scales
 
-        def multiply_piece(piece, on_vector, x, k_pass, bank, start, stop):
-            grouped = work.tile([P, QUARTER, PACK], BF16, align_bytes=64, name="grouped")
+        grouped_pieces = {}
+        quantised_pieces = {}
+        banks = {}
+        x_operands = {}
+
+        def regroup(n):
+            piece, on_vector, other_index, other_t = pieces[n]
+            grouped = work.tile(
+                [P, QUARTER, PACK], BF16, align_bytes=64, name="grouped", bufs=LEAD + 3
+            )
             copy = nc.vector.tensor_copy if on_vector else nc.scalar.copy
             copy(
                 out=grouped[:].rearrange("p (c i) j -> p c j i", i=4),
-                in_=piece.rearrange("p j (c i) -> p c j i", i=4),
+                in_=raw_pieces[piece].rearrange("p j (c i) -> p c j i", i=4),
             )
+            grouped_pieces[n] = grouped
+            if last_use[chunk_of(piece)] == n:
+                load_next_chunk()
+
+        def quantise(n):
             codes = work.tile([P, QUARTER], U32, align_bytes=64, name="codes")
             scales = work.tile([P, QUARTER], U8, align_bytes=64, name="scales")
             nc.vector.quantize_mx(
                 out=codes[:].bitcast(FP8X4),
                 scales=scales[:],
-                in_=grouped[:].rearrange("p w j -> p (w j)"),
+                in_=grouped_pieces[n][:].rearrange("p w j -> p (w j)"),
             )
-            x_codes, x_scales = x
+            quantised_pieces[n] = (codes, scales)
+
+        def multiply(n):
+            (matrix, k_pass, quarter), other_on, other_index, other_t = pieces[n]
+            lone = matrix in "kvq"
+            if lone or k_pass == 0:
+                bank = psum.tile([P, QUARTER], F32, name="bank", tag="bank")
+                banks[(matrix, quarter)] = bank
+            codes, scales = quantised_pieces[n]
+            x_codes, x_scales = x_operands["left" if matrix in "vo" else "conv"]
             batch = slice(k_pass * P, (k_pass + 1) * P)
             nc.tensor.matmul_mx(
-                out=bank[:],
+                out=banks[(matrix, quarter)][:],
                 lhsT=x_codes[:, batch].bitcast(FP8X4),
                 lhsT_scale=x_scales[:, batch],
                 rhs=codes[:].bitcast(FP8X4),
                 rhs_scale=scales[:],
-                start=start,
-                stop=stop,
+                start=lone or k_pass == 0,
+                stop=lone or k_pass == K_PASSES - 1,
             )
 
-        def multiply_dense(
-            weights, x, carried=None, after_first_chunk=None, piecewise_start=False
-        ):
-            banks = []
-            for k_pass in range(K_PASSES):
-                if piecewise_start and k_pass == 0:
-                    pieces = load_dense_piecewise(weights, k_pass)
-                else:
-                    pieces = load_dense(weights, k_pass)
-                for quarter in range(QUARTERS):
-                    if carried is not None:
-                        carried(quarter)
-                    if k_pass == 0:
-                        banks.append(psum.tile([P, QUARTER], F32, name="bank", tag="bank"))
-                    multiply_piece(
-                        pieces[quarter], carried is None and quarter % 2 == 0, x, k_pass,
-                        banks[quarter], start=(k_pass == 0), stop=(k_pass == K_PASSES - 1),
-                    )
-                if k_pass == 0 and after_first_chunk is not None:
-                    after_first_chunk()
-                carried = None
-            return banks
+        bias_turned = keep.tile([P, P], BF16, name="bias_turned")
+        bias = {}
+        bias_banks = {}
 
-        def multiply_heads(pieces, x, carried):
-            banks = []
-            for head in range(QUARTERS):
-                carried(head)
-                banks.append(psum.tile([P, QUARTER], F32, name="bank", tag="bank"))
-                multiply_piece(
-                    pieces[head], False, x, head,
-                    banks[head], start=True, stop=True,
+        def spread_bias(matrix, half):
+            first = list(bias_order).index(matrix) * BIAS_ROWS + half * BIAS_ROWS // 2
+            spread = psum.tile([P, HALF], BF16, name="spread", tag="bank")
+            for c in range(HALF // P):
+                nc.tensor.transpose(
+                    spread[:, c * P : (c + 1) * P],
+                    bias_turned[:, first + c : first + c + 1].to_broadcast([P, P]),
+                    identity_bf16[:],
                 )
-            return banks
+            bias_banks[(matrix, half)] = spread
 
-        i_gate = keep.tile([P, WIDTH], F32)
-        f_gate = keep.tile([P, WIDTH], F32)
-        m_t = keep.tile([P, WIDTH], F32)
-        n_t = keep.tile([P, WIDTH], F32)
-        c_t = keep.tile([P, WIDTH], F32)
-        ik = keep.tile([P, WIDTH], F32)
-        ikv = keep.tile([P, WIDTH], F32)
-        q = keep.tile([P, WIDTH], F32)
-        nq = keep.tile([P, WIDTH], F32)
-        h_t = keep.tile([P, WIDTH], F32)
-        squares = keep.tile([P, QUARTERS], F32)
-        norm = keep.tile([P, 1], F32)
-        half_over_denom = keep.tile([P, 1], F32)
-        one_half = keep.tile([P, 1], F32)
-        nc.vector.memset(one_half[:], 0.5)
-
-        xc = quantise_activations(load_rows([x_conv])[:, 0, :], "xc")
-        banks_i = multiply_dense(wi_w, xc, piecewise_start=True)
-        banks_f = multiply_dense(wf_w, xc)
-
-        pieces_k = load_heads(wk_w)
-        gate_rows = load_rows(
-            [wi_b.partition_broadcast(P), wf_b.partition_broadcast(P), m_prev, n_prev]
-        )
-        bias_i, bias_f, m_old, n_old = [gate_rows[:, slot, :] for slot in range(4)]
-        cell_rows = load_rows(
-            [c_prev, wk_b.partition_broadcast(P), x_left, wv_b.partition_broadcast(P)]
-        )
-        c_old, bias_k, x_left_rows, bias_v = [cell_rows[:, slot, :] for slot in range(4)]
-
-        nc.vector.tensor_tensor(out=f_gate[:], in0=bias_f, in1=m_old, op=ALU.add)
-
-        def finish_gates(quarter):
-            cols = columns(quarter)
-            nc.vector.tensor_tensor(
-                out=i_gate[:, cols], in0=banks_i[quarter][:], in1=bias_i[:, cols], op=ALU.add
+        def keep_bias(matrix, half):
+            if half == 0:
+                kept = keep.tile([P, WIDTH], BF16, name="bias_" + matrix)
+                bias[matrix] = kept
+            nc.scalar.copy(
+                out=bias[matrix][:, half * HALF : (half + 1) * HALF],
+                in_=bias_banks[(matrix, half)][:],
             )
+
+        gates = keep.tile([P, 2, WIDTH], F32, name="gates")
+        kv = keep.tile([P, 2, WIDTH], F32, name="kv")
+        nc_new = keep.tile([P, 2, WIDTH], F32, name="nc_new")
+        q = keep.tile([P, WIDTH], F32, name="q")
+        squares = keep.tile([P, QUARTERS], F32, name="squares")
+        norm = keep.tile([P, 1], F32, name="norm")
+        half_over_denom = keep.tile([P, 1], F32, name="half_over_denom")
+        temps = {}
+        scalar_queue = []
+        store_queue = []
+
+        def flush_scalar():
+            for run in scalar_queue:
+                run()
+            scalar_queue.clear()
+
+        def both(row):
+            return row.unsqueeze(1).to_broadcast([P, 2, QUARTER])
+
+        def add_bias(out, matrix, quarter):
             nc.vector.tensor_tensor(
-                out=f_gate[:, cols], in0=banks_f[quarter][:], in1=f_gate[:, cols], op=ALU.add
+                out=out, in0=banks[(matrix, quarter)][:], in1=bias[matrix][:, columns(quarter)],
+                op=ALU.add,
             )
+
+        def item_k(s):
+            add_bias(kv[:, 0, columns(s)], "k", s)
+
+        def item_v(s):
+            add_bias(kv[:, 1, columns(s)], "v", s)
+
+        def item_q(s):
+            add_bias(q[:, columns(s)], "q", s)
+
+        def item_vk(s):
             nc.vector.tensor_tensor(
-                out=m_t[:, cols], in0=i_gate[:, cols], in1=f_gate[:, cols], op=ALU.max
+                out=kv[:, 1, columns(s)], in0=kv[:, 1, columns(s)], in1=kv[:, 0, columns(s)],
+                op=ALU.mult,
             )
-            nc.gpsimd.dma_start(out=out_3[:, cols], in_=m_t[:, cols])
-            for gate in (i_gate, f_gate):
-                nc.vector.tensor_tensor(
-                    out=gate[:, cols], in0=gate[:, cols], in1=m_t[:, cols], op=ALU.subtract
+
+        def item_fm(half):
+            cols = slice(half * HALF, (half + 1) * HALF)
+            nc.vector.tensor_tensor(
+                out=gates[:, 1, cols], in0=bias_banks[("f", half)][:], in1=m_old[:, cols],
+                op=ALU.add,
+            )
+
+        def item_i(s):
+            add_bias(gates[:, 0, columns(s)], "i", s)
+
+        def item_f(s):
+            nc.vector.tensor_tensor(
+                out=gates[:, 1, columns(s)], in0=banks[("f", s)][:], in1=gates[:, 1, columns(s)],
+                op=ALU.add,
+            )
+
+        def item_max(s):
+            m_t = work.tile([P, QUARTER], F32, name="m_t")
+            temps[("m", s)] = m_t
+            nc.vector.tensor_tensor(
+                out=m_t[:], in0=gates[:, 0, columns(s)], in1=gates[:, 1, columns(s)], op=ALU.max
+            )
+            store_queue.append((out_3[:, columns(s)], m_t[:]))
+
+        def item_sub(s):
+            both_gates = gates[:, :, columns(s)]
+            nc.vector.tensor_tensor(
+                out=both_gates, in0=both_gates, in1=both(temps[("m", s)][:]), op=ALU.subtract
+            )
+
+            def exponentials():
+                nc.scalar.activation(out=both_gates, in_=both_gates, func=ACT.Exp)
+
+            scalar_queue.append(exponentials)
+
+        def item_ikv(s):
+            flush_scalar()
+            nc.vector.tensor_tensor(
+                out=kv[:, :, columns(s)], in0=kv[:, :, columns(s)],
+                in1=both(gates[:, 0, columns(s)]), op=ALU.mult,
+            )
+
+        def item_fnc(s):
+            nc.vector.tensor_tensor(
+                out=nc_new[:, :, columns(s)], in0=nc_old[:, :, columns(s)],
+                in1=both(gates[:, 1, columns(s)]), op=ALU.mult,
+            )
+
+        def item_nc(s):
+            nc.vector.scalar_tensor_tensor(
+                out=nc_new[:, :, columns(s)], in0=kv[:, :, columns(s)], scalar=K_SCALE,
+                in1=nc_new[:, :, columns(s)], op0=ALU.mult, op1=ALU.add,
+            )
+            store_queue.append((out_2[:, columns(s)], nc_new[:, 0, columns(s)]))
+            store_queue.append((out_1[:, columns(s)], nc_new[:, 1, columns(s)]))
+
+        def item_nq(s):
+            nq = work.tile([P, QUARTER], F32, name="nq", bufs=2)
+            nc.vector.tensor_tensor(
+                out=nq[:], in0=nc_new[:, 0, columns(s)], in1=q[:, columns(s)], op=ALU.mult
+            )
+
+            def square():
+                nc.scalar.activation(
+                    out=nq[:], in_=nq[:], func=ACT.Square, accum_out=squares[:, s : s + 1]
                 )
-                nc.scalar.activation(out=gate[:, cols], in_=gate[:, cols], func=ACT.Exp)
-            nc.vector.tensor_tensor(
-                out=n_t[:, cols], in0=f_gate[:, cols], in1=n_old[:, cols], op=ALU.mult
-            )
-            nc.vector.tensor_tensor(
-                out=c_t[:, cols], in0=f_gate[:, cols], in1=c_old[:, cols], op=ALU.mult
-            )
 
-        banks_k = multiply_heads(pieces_k, xc, finish_gates)
+            scalar_queue.append(square)
 
-        def finish_k(quarter):
-            cols = columns(quarter)
-            nc.vector.tensor_tensor(
-                out=ik[:, cols], in0=banks_k[quarter][:], in1=bias_k[:, cols], op=ALU.add
-            )
-            nc.vector.tensor_tensor(
-                out=ik[:, cols], in0=ik[:, cols], in1=i_gate[:, cols], op=ALU.mult
-            )
-            nc.vector.scalar_tensor_tensor(
-                out=n_t[:, cols], in0=ik[:, cols], scalar=K_SCALE, in1=n_t[:, cols],
-                op0=ALU.mult, op1=ALU.add,
-            )
-            nc.gpsimd.dma_start(out=out_2[:, cols], in_=n_t[:, cols])
-
-        pieces_v = load_heads(wv_w)
-        xl = quantise_activations(x_left_rows, "xl")
-        banks_v = multiply_heads(pieces_v, xl, finish_k)
-
-        def finish_v(quarter):
-            cols = columns(quarter)
-            nc.vector.tensor_tensor(
-                out=ikv[:, cols], in0=banks_v[quarter][:], in1=bias_v[:, cols], op=ALU.add
-            )
-            nc.vector.tensor_tensor(
-                out=ikv[:, cols], in0=ikv[:, cols], in1=ik[:, cols], op=ALU.mult
-            )
-            nc.vector.scalar_tensor_tensor(
-                out=c_t[:, cols], in0=ikv[:, cols], scalar=K_SCALE, in1=c_t[:, cols],
-                op0=ALU.mult, op1=ALU.add,
-            )
-            nc.gpsimd.dma_start(out=out_1[:, cols], in_=c_t[:, cols])
-
-        pieces_q = load_heads(wq_w)
-        last_rows = load_rows([wq_b.partition_broadcast(P), wo_b.partition_broadcast(P)])
-        bias_q, bias_o = [last_rows[:, slot, :] for slot in range(2)]
-        banks_q = multiply_heads(pieces_q, xc, finish_v)
-
-        def finish_q(quarter):
-            cols = columns(quarter)
-            nc.vector.tensor_tensor(
-                out=q[:, cols], in0=banks_q[quarter][:], in1=bias_q[:, cols], op=ALU.add
-            )
-            nc.vector.tensor_tensor(
-                out=nq[:, cols], in0=n_t[:, cols], in1=q[:, cols], op=ALU.mult
-            )
-            nc.scalar.activation(
-                out=nq[:, cols], in_=nq[:, cols], func=ACT.Square,
-                accum_out=squares[:, quarter : quarter + 1],
-            )
-
-        def normalise():
+        def item_sum(other_s):
+            flush_scalar()
             nc.vector.reduce_sum(out=norm[:], in_=squares[:], axis=mybir.AxisListType.X)
             nc.gpsimd.tensor_tensor(out=norm[:], in0=norm[:], in1=one_half[:], op=ALU.pow)
+
+        def item_denom(other_s):
             nc.vector.tensor_scalar(
                 out=norm[:], in0=norm[:], scalar1=2.0, scalar2=2.0 * EPSILON,
                 op0=ALU.mult, op1=ALU.add,
             )
-            nc.vector.reciprocal(out=half_over_denom[:], in_=norm[:])
-            for quarter in range(QUARTERS):
-                cols = columns(quarter)
-                nc.vector.scalar_tensor_tensor(
-                    out=q[:, cols], in0=c_t[:, cols], scalar=half_over_denom[:, 0:1],
-                    in1=q[:, cols], op0=ALU.mult, op1=ALU.mult,
-                )
 
-        banks_o = multiply_dense(
-            wo_w, xl, carried=finish_q, after_first_chunk=normalise
-        )
-        for quarter in range(QUARTERS):
-            cols = columns(quarter)
-            nc.vector.tensor_tensor(
-                out=h_t[:, cols], in0=banks_o[quarter][:], in1=bias_o[:, cols], op=ALU.add
-            )
-            nc.scalar.activation(out=h_t[:, cols], in_=h_t[:, cols], func=ACT.Tanh, scale=0.5)
+        def item_reciprocal(other_s):
+            nc.vector.reciprocal(out=half_over_denom[:], in_=norm[:])
+
+        def item_cq(s):
             nc.vector.scalar_tensor_tensor(
-                out=h_t[:, cols], in0=h_t[:, cols], scalar=1.0, in1=q[:, cols],
+                out=q[:, columns(s)], in0=nc_new[:, 1, columns(s)],
+                scalar=half_over_denom[:, 0:1], in1=q[:, columns(s)], op0=ALU.mult, op1=ALU.mult,
+            )
+
+        def item_o(s):
+            h_t = work.tile([P, QUARTER], F32, name="h_t")
+            temps[("h", s)] = h_t
+            add_bias(h_t[:], "o", s)
+
+            def tanh():
+                nc.scalar.activation(out=h_t[:], in_=h_t[:], func=ACT.Tanh, scale=0.5)
+
+            scalar_queue.append(tanh)
+
+        def item_h(s):
+            flush_scalar()
+            h_t = temps[("h", s)]
+            nc.vector.scalar_tensor_tensor(
+                out=h_t[:], in0=h_t[:], scalar=1.0, in1=q[:, columns(s)],
                 op0=ALU.add, op1=ALU.mult,
             )
-            nc.sync.dma_start(out=out_0[:, cols], in_=h_t[:, cols])
+            store_queue.append((out_0[:, columns(s)], h_t[:]))
+
+        def update(a, b):
+            return [
+                (1, item_f, a), (1, item_f, b), (1, item_max, a), (1, item_max, b),
+                (2, item_sub, a), (2, item_sub, b), (1, item_vk, a), (1, item_vk, b),
+                (2, item_ikv, a), (2, item_fnc, a), (2, item_ikv, b), (2, item_fnc, b),
+                (2, item_nc, a), (2, item_nc, b), (1, item_nq, a), (1, item_nq, b),
+            ]
+
+        first_update = update(0, 1) + [(1, item_i, 2), (1, item_i, 3)]
+        last_update = update(2, 3) + [
+            (1, item_o, 0), (1, item_o, 1),
+            (1, item_sum, 0), (1, item_denom, 0), (1, item_reciprocal, 0),
+            (1, item_cq, 0), (1, item_cq, 1), (1, item_cq, 2), (1, item_cq, 3),
+            (1, item_o, 2), (1, item_h, 0), (1, item_h, 1),
+        ]
+        carried = [
+            (0, 1, 0, [(1, item_k, s) for s in range(4)] + [(1, item_v, s) for s in range(4)]
+                + [(1, item_q, s) for s in range(2)]),
+            (1, 1, 0, [(1, item_q, 2), (1, item_q, 3), (2, item_fm, 0), (2, item_fm, 1)]),
+            (2, 1, 0, [(1, item_i, 0), (1, item_i, 1)]),
+            (3, 2, 0, first_update),
+            (5, 2, 2, last_update),
+        ]
+        items_of_step = []
+        for first, count, spare, items in carried:
+            steps = sum(len(stages[first + n]) for n in range(count))
+            total = sum(units for units, other_item, other_s in items)
+            plan = [[] for other_step in range(steps)]
+            offset = 0
+            for units, item, s in items:
+                step = min(steps - 1, (offset + units) * (steps - spare) // total)
+                plan[step].append((item, s))
+                offset += units
+            items_of_step.extend(plan)
+
+        def flush_stores():
+            for target, source in store_queue:
+                nc.sync.dma_start(out=target, in_=source)
+            store_queue.clear()
+
+        grouped_conv = turn_activations(x_conv_rows, nc.vector.tensor_copy)
+        turned_bias = psum.tile([P, P], BF16, name="turned_bias", tag="bank")
+        nc.tensor.transpose(turned_bias[:], bias_rows[:], identity_bf16[:])
+        nc.vector.tensor_copy(out=bias_turned[:], in_=turned_bias[:])
+        for n in range(LEAD):
+            regroup(n)
+        x_operands["conv"] = quantise_activations(grouped_conv, "x_conv")
+        spread_bias("k", 0)
+        keep_bias("k", 0)
+        bias_jobs = [("k", 1)] + [(m, h) for m in ("v", "q", "i", "o") for h in range(2)]
+        grouped_left = None
+
+        for n in range(len(pieces)):
+            quantise(n)
+            if n + LEAD < len(pieces):
+                regroup(n + LEAD)
+            if n == 1:
+                grouped_left = turn_activations(x_left_rows, nc.scalar.copy)
+            if n == 3:
+                x_operands["left"] = quantise_activations(grouped_left, "x_left")
+            if n < len(bias_jobs):
+                spread_bias(*bias_jobs[n])
+            if n in (10, 11):
+                spread_bias("f", n - 10)
+            multiply(n)
+            flush_scalar()
+            if n < len(bias_jobs):
+                keep_bias(*bias_jobs[n])
+            flush_stores()
+            for item, s in items_of_step[n]:
+                item(s)
+        flush_scalar()
+        item_o(3)
+        item_h(2)
+        item_h(3)
+        flush_stores()

@@ -65,7 +65,7 @@ def tile_mlstmblock_pb_kernel(
                 )
         stages.append([("o", k, s) for k in range(K_PASSES) for s in range(2)])
         stages.append([("o", k, 2 + s) for s in range(2) for k in range(K_PASSES)])
-        on_vector_counts = [6, 3, 4, 2, 2, 2, 2]
+        on_vector_counts = [6, 3, 4, 2, 2, 2, 1]
         pieces = []
         for index, stage in enumerate(stages):
             for t, piece in enumerate(stage):
@@ -124,13 +124,13 @@ def tile_mlstmblock_pb_kernel(
         nc_old = keep.tile([P, 2, WIDTH], BF16, name="nc_old")
         bias_rows = keep.tile([P, P], BF16, name="bias_rows")
         nc.gpsimd.memset(bias_rows[96:P, :], 0.0)
+        nc.sync.dma_start(out=x_conv_rows[:], in_=x_conv)
+        load_next_chunk()
         for r, matrix in enumerate(bias_order):
-            nc.gpsimd.dma_start(
+            nc.sync.dma_start(
                 out=bias_rows[r * BIAS_ROWS : (r + 1) * BIAS_ROWS, :],
                 in_=bias_order[matrix].rearrange("(c n) -> c n", n=P),
             )
-        nc.sync.dma_start(out=x_conv_rows[:], in_=x_conv)
-        load_next_chunk()
         load_next_chunk()
         nc.sync.dma_start(out=x_left_rows[:], in_=x_left)
         for other_more in range(RING - 2):
@@ -261,6 +261,9 @@ def tile_mlstmblock_pb_kernel(
                 out=out, in0=banks[(matrix, quarter)][:], in1=bias[matrix][:, columns(quarter)],
                 op=ALU.add,
             )
+
+        def item_none(other_s):
+            return
 
         def item_k(s):
             add_bias(kv[:, 0, columns(s)], "k", s)
@@ -401,7 +404,7 @@ def tile_mlstmblock_pb_kernel(
             (1, item_o, 2), (1, item_h, 0), (1, item_h, 1),
         ]
         carried = [
-            (0, 1, 0, [(1, item_k, s) for s in range(4)] + [(1, item_v, s) for s in range(4)]
+            (0, 1, 0, [(2, item_none, 0)] + [(1, item_k, s) for s in range(4)] + [(1, item_v, s) for s in range(4)]
                 + [(1, item_q, s) for s in range(2)]),
             (1, 1, 0, [(1, item_q, 2), (1, item_q, 3), (2, item_fm, 0), (2, item_fm, 1)]),
             (2, 1, 0, [(1, item_i, 0), (1, item_i, 1)]),
@@ -426,21 +429,20 @@ def tile_mlstmblock_pb_kernel(
             store_queue.clear()
 
         grouped_conv = turn_activations(x_conv_rows, nc.vector.tensor_copy)
-        turned_bias = psum.tile([P, P], BF16, name="turned_bias", tag="bank")
-        nc.tensor.transpose(turned_bias[:], bias_rows[:], identity_bf16[:])
-        nc.vector.tensor_copy(out=bias_turned[:], in_=turned_bias[:])
         for n in range(LEAD):
             regroup(n)
         x_operands["conv"] = quantise_activations(grouped_conv, "x_conv")
-        spread_bias("k", 0)
-        keep_bias("k", 0)
-        bias_jobs = [("k", 1)] + [(m, h) for m in ("v", "q", "i", "o") for h in range(2)]
+        bias_jobs = [(m, h) for m in ("k", "v", "q", "i", "o") for h in range(2)]
         grouped_left = None
 
         for n in range(len(pieces)):
             quantise(n)
             if n + LEAD < len(pieces):
                 regroup(n + LEAD)
+            if n == 0:
+                turned_bias = psum.tile([P, P], BF16, name="turned_bias", tag="bank")
+                nc.tensor.transpose(turned_bias[:], bias_rows[:], identity_bf16[:])
+                nc.vector.tensor_copy(out=bias_turned[:], in_=turned_bias[:])
             if n == 1:
                 grouped_left = turn_activations(x_left_rows, nc.scalar.copy)
             if n == 3:

@@ -23,6 +23,7 @@ K_PASSES = WIDTH // K_PASS
 BIAS_ROWS = WIDTH // P
 
 RING = 9
+THROUGH_TENSOR = ((2, 2), (3, 2), (4, 2), (5, 1), (5, 4), (6, 1))
 LEAD = 2
 PSUM_BANKS = 8
 
@@ -70,15 +71,19 @@ def tile_mlstmblock_pb_kernel(
         for index, stage in enumerate(stages):
             for t, piece in enumerate(stage):
                 share = on_vector_counts[index]
-                on_vector = (t + 1) * share // len(stage) > t * share // len(stage)
-                pieces.append((piece, on_vector, index, t))
+                where = "scalar"
+                if (t + 1) * share // len(stage) > t * share // len(stage):
+                    where = "vector"
+                elif (index, t) in THROUGH_TENSOR:
+                    where = "tensor"
+                pieces.append((piece, where))
 
         def chunk_of(piece):
             matrix, k_pass, quarter = piece
             return (matrix, quarter // 2) if matrix in "kvq" else (matrix, k_pass, quarter // 2)
 
         chunk_order = []
-        for piece, other_on, other_index, other_t in pieces:
+        for piece, other_where in pieces:
             if chunk_of(piece) not in chunk_order:
                 chunk_order.append(chunk_of(piece))
         last_use = {chunk_of(entry[0]): n for n, entry in enumerate(pieces)}
@@ -170,16 +175,45 @@ def tile_mlstmblock_pb_kernel(
         banks = {}
         x_operands = {}
 
+        ordered_pieces = {}
+
+        def order(n):
+            piece, where = pieces[n]
+            if where != "tensor":
+                return
+            ordered_pieces[n] = []
+            for part in range(2):
+                ordered = psum.tile([P, 2 * QUARTER], BF16, name="ordered", tag="bank")
+                ordered_pieces[n].append(ordered)
+                for s in range(2):
+                    first = (2 * part + s) * P
+                    nc.tensor.matmul(
+                        out=ordered[:, columns(s)],
+                        lhsT=identity_bf16[:],
+                        rhs=raw_pieces[piece][:, :, first : first + P].rearrange("p j c -> p c j"),
+                        start=True,
+                        stop=True,
+                    )
+
         def regroup(n):
-            piece, on_vector, other_index, other_t = pieces[n]
+            piece, where = pieces[n]
             grouped = work.tile(
                 [P, QUARTER, PACK], BF16, align_bytes=64, name="grouped", bufs=LEAD + 3
             )
-            copy = nc.vector.tensor_copy if on_vector else nc.scalar.copy
-            copy(
-                out=grouped[:].rearrange("p (c i) j -> p c j i", i=4),
-                in_=raw_pieces[piece].rearrange("p j (c i) -> p c j i", i=4),
-            )
+            if where == "tensor":
+                for part, ordered in enumerate(ordered_pieces[n]):
+                    nc.scalar.copy(
+                        out=grouped[:, part * 2 * P : (part + 1) * 2 * P, :].rearrange(
+                            "p c j -> p (c j)"
+                        ),
+                        in_=ordered[:],
+                    )
+            else:
+                copy = nc.vector.tensor_copy if where == "vector" else nc.scalar.copy
+                copy(
+                    out=grouped[:].rearrange("p (c i) j -> p c j i", i=4),
+                    in_=raw_pieces[piece].rearrange("p j (c i) -> p c j i", i=4),
+                )
             grouped_pieces[n] = grouped
             if last_use[chunk_of(piece)] == n:
                 load_next_chunk()
@@ -195,7 +229,7 @@ def tile_mlstmblock_pb_kernel(
             quantised_pieces[n] = (codes, scales)
 
         def multiply(n):
-            (matrix, k_pass, quarter), other_on, other_index, other_t = pieces[n]
+            (matrix, k_pass, quarter), other_where = pieces[n]
             lone = matrix in "kvq"
             if lone or k_pass == 0:
                 bank = psum.tile([P, QUARTER], F32, name="bank", tag="bank")
@@ -274,12 +308,6 @@ def tile_mlstmblock_pb_kernel(
         def item_q(s):
             add_bias(q[:, columns(s)], "q", s)
 
-        def item_vk(s):
-            nc.vector.tensor_tensor(
-                out=kv[:, 1, columns(s)], in0=kv[:, 1, columns(s)], in1=kv[:, 0, columns(s)],
-                op=ALU.mult,
-            )
-
         def item_fm(half):
             cols = slice(half * HALF, (half + 1) * HALF)
             nc.vector.tensor_tensor(
@@ -315,14 +343,21 @@ def tile_mlstmblock_pb_kernel(
 
             scalar_queue.append(exponentials)
 
-        def item_ikv(s):
+        def item_ik(s):
             flush_scalar()
             nc.vector.tensor_tensor(
-                out=kv[:, :, columns(s)], in0=kv[:, :, columns(s)],
-                in1=both(gates[:, 0, columns(s)]), op=ALU.mult,
+                out=kv[:, 0, columns(s)], in0=kv[:, 0, columns(s)], in1=gates[:, 0, columns(s)],
+                op=ALU.mult,
+            )
+
+        def item_ikv(s):
+            nc.vector.tensor_tensor(
+                out=kv[:, 1, columns(s)], in0=kv[:, 1, columns(s)], in1=kv[:, 0, columns(s)],
+                op=ALU.mult,
             )
 
         def item_fnc(s):
+            flush_scalar()
             nc.vector.tensor_tensor(
                 out=nc_new[:, :, columns(s)], in0=nc_old[:, :, columns(s)],
                 in1=both(gates[:, 1, columns(s)]), op=ALU.mult,
@@ -391,8 +426,8 @@ def tile_mlstmblock_pb_kernel(
         def update(a, b):
             return [
                 (1, item_f, a), (1, item_f, b), (1, item_max, a), (1, item_max, b),
-                (2, item_sub, a), (2, item_sub, b), (1, item_vk, a), (1, item_vk, b),
-                (2, item_ikv, a), (2, item_fnc, a), (2, item_ikv, b), (2, item_fnc, b),
+                (2, item_sub, a), (2, item_sub, b), (2, item_fnc, a), (1, item_ik, a),
+                (2, item_fnc, b), (1, item_ik, b), (1, item_ikv, a), (1, item_ikv, b),
                 (2, item_nc, a), (2, item_nc, b), (1, item_nq, a), (1, item_nq, b),
             ]
 
@@ -437,6 +472,8 @@ def tile_mlstmblock_pb_kernel(
 
         for n in range(len(pieces)):
             quantise(n)
+            if n + LEAD + 1 < len(pieces):
+                order(n + LEAD + 1)
             if n + LEAD < len(pieces):
                 regroup(n + LEAD)
             if n == 0:

@@ -23,7 +23,6 @@ K_PASSES = WIDTH // K_PASS
 BIAS_ROWS = WIDTH // P
 
 RING = 9
-THROUGH_TENSOR = ((2, 2), (3, 2), (4, 2), (5, 1), (5, 4), (6, 1))
 LEAD = 2
 PSUM_BANKS = 8
 
@@ -66,7 +65,7 @@ def tile_mlstmblock_pb_kernel(
                 )
         stages.append([("o", k, s) for k in range(K_PASSES) for s in range(2)])
         stages.append([("o", k, 2 + s) for s in range(2) for k in range(K_PASSES)])
-        on_vector_counts = [6, 3, 4, 2, 2, 2, 1]
+        on_vector_counts = [6, 4, 4, 3, 3, 2, 1]
         pieces = []
         for index, stage in enumerate(stages):
             for t, piece in enumerate(stage):
@@ -74,8 +73,6 @@ def tile_mlstmblock_pb_kernel(
                 where = "scalar"
                 if (t + 1) * share // len(stage) > t * share // len(stage):
                     where = "vector"
-                elif (index, t) in THROUGH_TENSOR:
-                    where = "tensor"
                 pieces.append((piece, where))
 
         def chunk_of(piece):
@@ -123,14 +120,26 @@ def tile_mlstmblock_pb_kernel(
         nc.vector.memset(one_half[:], 0.5)
         nc.scalar.activation(out=warm[:], in_=one_half[:], func=ACT.Exp)
 
+        def load_first_chunk_and_x_conv():
+            chunk = chunk_order[0]
+            loaded.append(chunk)
+            raw = ring.tile([P, 2, PACK * QUARTER], BF16, name="raw_heads", tag="ring")
+            for s in range(2):
+                cols = slice(s * HALF, (s + 1) * HALF)
+                nc.sync.dma_start(out=x_conv_rows[:, cols], in_=x_conv[:, cols])
+                nc.sync.dma_start(
+                    out=raw[:, s, :],
+                    in_=wk_w.rearrange("h (p j) o -> p h (j o)", j=PACK)[:, s, :],
+                )
+                raw_pieces[("k", s, s)] = raw[:, s, :].rearrange("p (j o) -> p j o", j=PACK)
+
         x_conv_rows = keep.tile([P, WIDTH], BF16, name="x_conv_rows")
         x_left_rows = keep.tile([P, WIDTH], BF16, name="x_left_rows")
         m_old = keep.tile([P, WIDTH], BF16, name="m_old")
         nc_old = keep.tile([P, 2, WIDTH], BF16, name="nc_old")
         bias_rows = keep.tile([P, P], BF16, name="bias_rows")
         nc.gpsimd.memset(bias_rows[96:P, :], 0.0)
-        nc.sync.dma_start(out=x_conv_rows[:], in_=x_conv)
-        load_next_chunk()
+        load_first_chunk_and_x_conv()
         for r, matrix in enumerate(bias_order):
             nc.sync.dma_start(
                 out=bias_rows[r * BIAS_ROWS : (r + 1) * BIAS_ROWS, :],
@@ -147,73 +156,47 @@ def tile_mlstmblock_pb_kernel(
         identity_bf16 = keep.tile([P, P], BF16, name="identity_bf16")
         nc.vector.tensor_copy(out=identity_bf16[:], in_=identity[:])
 
-        def turn_activations(x_rows, copy_out):
+        x_operands = {}
+
+        def turn_activations(x_rows, name, half, copy_out):
             words = x_rows[:].bitcast(F32).rearrange("b (c p u) -> b c u p", p=P, u=2)
-            grouped = work.tile([P, WIDTH], BF16, align_bytes=64, name="x_grouped", bufs=1)
-            grouped_words = grouped[:].bitcast(F32).rearrange("p (c b u) -> p c b u", b=P, u=2)
-            for half in range(2):
-                turned = psum.tile([P, 2, 2, P], F32, name="turned", tag="bank")
-                for c in range(2):
-                    for u in range(2):
-                        nc.tensor.transpose(
-                            turned[:, c, u, :], words[:, 2 * half + c, u, :], identity[:]
-                        )
-                copy_out(
-                    out=grouped_words[:, 2 * half : 2 * half + 2, :, :],
-                    in_=turned[:].rearrange("p c u b -> p c b u"),
-                )
+            grouped = work.tile([P, HALF], BF16, align_bytes=64, name="x_grouped", bufs=2)
+            turned = psum.tile([P, 2, 2, P], F32, name="turned", tag="bank")
+            for c in range(2):
+                for u in range(2):
+                    nc.tensor.transpose(
+                        turned[:, c, u, :], words[:, 2 * half + c, u, :], identity[:]
+                    )
+            copy_out(
+                out=grouped[:].bitcast(F32).rearrange("p (c b u) -> p c b u", b=P, u=2),
+                in_=turned[:].rearrange("p c u b -> p c b u"),
+            )
+            if half == 0:
+                codes = keep.tile([P, K_PASSES * P], U32, align_bytes=64, name=name + "_codes")
+                scales = keep.tile([P, K_PASSES * P], U8, align_bytes=64, name=name + "_scales")
+                x_operands[name] = (codes, scales)
             return grouped
 
-        def quantise_activations(grouped, name):
-            codes = keep.tile([P, K_PASSES * P], U32, align_bytes=64, name=name + "_codes")
-            scales = keep.tile([P, K_PASSES * P], U8, align_bytes=64, name=name + "_scales")
-            nc.vector.quantize_mx(out=codes[:].bitcast(FP8X4), scales=scales[:], in_=grouped[:])
-            return codes, scales
+        def quantise_activations(grouped, name, half):
+            codes, scales = x_operands[name]
+            batch = slice(half * 2 * P, (half + 1) * 2 * P)
+            nc.vector.quantize_mx(
+                out=codes[:, batch].bitcast(FP8X4), scales=scales[:, batch], in_=grouped[:]
+            )
 
         grouped_pieces = {}
         quantised_pieces = {}
         banks = {}
-        x_operands = {}
-
-        ordered_pieces = {}
-
-        def order(n):
-            piece, where = pieces[n]
-            if where != "tensor":
-                return
-            ordered_pieces[n] = []
-            for part in range(2):
-                ordered = psum.tile([P, 2 * QUARTER], BF16, name="ordered", tag="bank")
-                ordered_pieces[n].append(ordered)
-                for s in range(2):
-                    first = (2 * part + s) * P
-                    nc.tensor.matmul(
-                        out=ordered[:, columns(s)],
-                        lhsT=identity_bf16[:],
-                        rhs=raw_pieces[piece][:, :, first : first + P].rearrange("p j c -> p c j"),
-                        start=True,
-                        stop=True,
-                    )
-
         def regroup(n):
             piece, where = pieces[n]
             grouped = work.tile(
                 [P, QUARTER, PACK], BF16, align_bytes=64, name="grouped", bufs=LEAD + 3
             )
-            if where == "tensor":
-                for part, ordered in enumerate(ordered_pieces[n]):
-                    nc.scalar.copy(
-                        out=grouped[:, part * 2 * P : (part + 1) * 2 * P, :].rearrange(
-                            "p c j -> p (c j)"
-                        ),
-                        in_=ordered[:],
-                    )
-            else:
-                copy = nc.vector.tensor_copy if where == "vector" else nc.scalar.copy
-                copy(
-                    out=grouped[:].rearrange("p (c i) j -> p c j i", i=4),
-                    in_=raw_pieces[piece].rearrange("p j (c i) -> p c j i", i=4),
-                )
+            copy = nc.vector.tensor_copy if where == "vector" else nc.scalar.copy
+            copy(
+                out=grouped[:].rearrange("p (c i) j -> p c j i", i=4),
+                in_=raw_pieces[piece].rearrange("p j (c i) -> p c j i", i=4),
+            )
             grouped_pieces[n] = grouped
             if last_use[chunk_of(piece)] == n:
                 load_next_chunk()
@@ -463,17 +446,15 @@ def tile_mlstmblock_pb_kernel(
                 nc.sync.dma_start(out=target, in_=source)
             store_queue.clear()
 
-        grouped_conv = turn_activations(x_conv_rows, nc.vector.tensor_copy)
+        for half in range(2):
+            grouped_conv = turn_activations(x_conv_rows, "conv", half, nc.vector.tensor_copy)
+            quantise_activations(grouped_conv, "conv", half)
         for n in range(LEAD):
             regroup(n)
-        x_operands["conv"] = quantise_activations(grouped_conv, "x_conv")
         bias_jobs = [(m, h) for m in ("k", "v", "q", "i", "o") for h in range(2)]
-        grouped_left = None
 
         for n in range(len(pieces)):
             quantise(n)
-            if n + LEAD + 1 < len(pieces):
-                order(n + LEAD + 1)
             if n + LEAD < len(pieces):
                 regroup(n + LEAD)
             if n == 0:
@@ -481,9 +462,13 @@ def tile_mlstmblock_pb_kernel(
                 nc.tensor.transpose(turned_bias[:], bias_rows[:], identity_bf16[:])
                 nc.vector.tensor_copy(out=bias_turned[:], in_=turned_bias[:])
             if n == 1:
-                grouped_left = turn_activations(x_left_rows, nc.scalar.copy)
+                grouped_left = [
+                    turn_activations(x_left_rows, "left", half, nc.scalar.copy)
+                    for half in range(2)
+                ]
             if n == 3:
-                x_operands["left"] = quantise_activations(grouped_left, "x_left")
+                for half in range(2):
+                    quantise_activations(grouped_left[half], "left", half)
             if n < len(bias_jobs):
                 spread_bias(*bias_jobs[n])
             if n in (10, 11):
@@ -496,7 +481,22 @@ def tile_mlstmblock_pb_kernel(
             for item, s in items_of_step[n]:
                 item(s)
         flush_scalar()
-        item_o(3)
+        h_t = work.tile([P, QUARTER], F32, name="h_t")
+        for part in range(2):
+            cols = slice(part * QUARTER // 2, (part + 1) * QUARTER // 2)
+            wide = slice(3 * QUARTER + cols.start, 3 * QUARTER + cols.stop)
+            nc.vector.tensor_tensor(
+                out=h_t[:, cols], in0=banks[("o", 3)][:, cols], in1=bias["o"][:, wide],
+                op=ALU.add,
+            )
+            nc.scalar.activation(out=h_t[:, cols], in_=h_t[:, cols], func=ACT.Tanh, scale=0.5)
         item_h(2)
-        item_h(3)
         flush_stores()
+        for part in range(2):
+            cols = slice(part * QUARTER // 2, (part + 1) * QUARTER // 2)
+            wide = slice(3 * QUARTER + cols.start, 3 * QUARTER + cols.stop)
+            nc.vector.scalar_tensor_tensor(
+                out=h_t[:, cols], in0=h_t[:, cols], scalar=1.0, in1=q[:, wide],
+                op0=ALU.add, op1=ALU.mult,
+            )
+            nc.sync.dma_start(out=out_0[:, wide], in_=h_t[:, cols])

@@ -22,6 +22,7 @@ HALF = 2 * QUARTER
 K_PASSES = WIDTH // K_PASS
 BIAS_ROWS = WIDTH // P
 
+RUN = 2
 RING = 9
 LEAD = 2
 PSUM_BANKS = 8
@@ -194,8 +195,8 @@ def tile_mlstmblock_pb_kernel(
             )
             copy = nc.vector.tensor_copy if where == "vector" else nc.scalar.copy
             copy(
-                out=grouped[:].rearrange("p (c i) j -> p c j i", i=4),
-                in_=raw_pieces[piece].rearrange("p j (c i) -> p c j i", i=4),
+                out=grouped[:].rearrange("p (c i) j -> p c j i", i=RUN),
+                in_=raw_pieces[piece].rearrange("p j (c i) -> p c j i", i=RUN),
             )
             grouped_pieces[n] = grouped
             if last_use[chunk_of(piece)] == n:

@@ -23,14 +23,19 @@ K_PASSES = WIDTH // K_PASS
 BIAS_ROWS = WIDTH // P
 
 RUN = 2
-RING = 9
+RING = 7
 LEAD = 2
+GROUPED = 4
 PSUM_BANKS = 8
 
 K_SCALE = 1.0 / math.sqrt(QUARTER)
 EPSILON = 1e-6
 
 FLOPS = 2 * P * (3 * WIDTH * WIDTH + 3 * QUARTERS * QUARTER * QUARTER)
+
+
+def half_columns(half):
+    return slice(half * HALF, (half + 1) * HALF)
 
 
 def columns(quarter):
@@ -57,61 +62,64 @@ def tile_mlstmblock_pb_kernel(
         make_identity(nc, identity[:])
         ctx.enter_context(tc.manual_schedule())
 
-        stages = []
-        stages.append([(m, head, head) for m in ("k", "v", "q") for head in range(QUARTERS)])
-        for half in range(2):
-            for m in ("i", "f"):
-                stages.append(
-                    [(m, k, 2 * half + s) for k in range(K_PASSES) for s in range(2)]
-                )
-        stages.append([("o", k, s) for k in range(K_PASSES) for s in range(2)])
-        stages.append([("o", k, 2 + s) for s in range(2) for k in range(K_PASSES)])
-        on_vector_counts = [6, 4, 4, 3, 3, 2, 1]
-        pieces = []
-        for index, stage in enumerate(stages):
-            for t, piece in enumerate(stage):
-                share = on_vector_counts[index]
-                where = "scalar"
-                if (t + 1) * share // len(stage) > t * share // len(stage):
-                    where = "vector"
-                pieces.append((piece, where))
+        def pair(matrix, k_pass, half):
+            if matrix in "kvq":
+                return [(matrix, 2 * half + s, 2 * half + s) for s in range(2)]
+            return [(matrix, k_pass, 2 * half + s) for s in range(2)]
+
+        stages = [[pair(matrix, None, half) for matrix in "kvq" for half in range(2)]]
+        for matrix, half in (("i", 0), ("f", 0), ("i", 1), ("f", 1), ("o", 0), ("o", 1)):
+            stages.append([pair(matrix, k_pass, half) for k_pass in range(K_PASSES)])
+        stages[0][0:1] = [[piece] for piece in stages[0][0]]
+        stages[-1][-1:] = [[piece] for piece in stages[-1][-1]]
+
+        on_vector_counts = [6, 4, 4, 3, 3, 2, 0]
+        units = []
+        for stage, share in zip(stages, on_vector_counts):
+            count = sum(len(unit) for unit in stage)
+            t = 0
+            for unit in stage:
+                flags = []
+                for piece in unit:
+                    flags.append((t + 1) * share // count > t * share // count)
+                    t += 1
+                units.append((unit, flags))
 
         def chunk_of(piece):
             matrix, k_pass, quarter = piece
-            return (matrix, quarter // 2) if matrix in "kvq" else (matrix, k_pass, quarter // 2)
+            return (matrix, None if matrix in "kvq" else k_pass, quarter // 2)
 
         chunk_order = []
-        for piece, other_where in pieces:
-            if chunk_of(piece) not in chunk_order:
-                chunk_order.append(chunk_of(piece))
-        last_use = {chunk_of(entry[0]): n for n, entry in enumerate(pieces)}
+        for unit, flags in units:
+            if chunk_of(unit[0]) not in chunk_order:
+                chunk_order.append(chunk_of(unit[0]))
+        left = {chunk: 2 for chunk in chunk_order}
 
         raw_pieces = {}
         loaded = []
 
-        def load_next_chunk():
+        def load_next_chunk(before_piece=None):
             if len(loaded) == len(chunk_order):
                 return
-            chunk = chunk_order[len(loaded)]
-            loaded.append(chunk)
-            source = weights[chunk[0]]
-            if len(chunk) == 2:
+            matrix, k_pass, half = chunk_order[len(loaded)]
+            loaded.append(half)
+            source = weights[matrix]
+            if matrix in "kvq":
                 raw = ring.tile([P, 2, PACK * QUARTER], BF16, name="raw_heads", tag="ring")
                 for s in range(2):
-                    head = 2 * chunk[1] + s
+                    head = 2 * half + s
+                    if before_piece is not None:
+                        before_piece(s)
                     nc.sync.dma_start(
                         out=raw[:, s, :],
                         in_=source.rearrange("h (p j) o -> p h (j o)", j=PACK)[:, head, :],
                     )
-                    raw_pieces[(chunk[0], head, head)] = raw[:, s, :].rearrange(
+                    raw_pieces[(matrix, head, head)] = raw[:, s, :].rearrange(
                         "p (j o) -> p j o", j=PACK
                     )
             else:
-                matrix, k_pass, half = chunk
                 raw = ring.tile([P, PACK, HALF], BF16, name="raw_dense", tag="ring")
-                rows = source[
-                    k_pass * K_PASS : (k_pass + 1) * K_PASS, half * HALF : (half + 1) * HALF
-                ]
+                rows = source[k_pass * K_PASS : (k_pass + 1) * K_PASS, half_columns(half)]
                 nc.sync.dma_start(out=raw[:], in_=rows.rearrange("(p j) n -> p j n", j=PACK))
                 for s in range(2):
                     raw_pieces[(matrix, k_pass, 2 * half + s)] = raw[:, :, columns(s)]
@@ -121,26 +129,19 @@ def tile_mlstmblock_pb_kernel(
         nc.vector.memset(one_half[:], 0.5)
         nc.scalar.activation(out=warm[:], in_=one_half[:], func=ACT.Exp)
 
-        def load_first_chunk_and_x_conv():
-            chunk = chunk_order[0]
-            loaded.append(chunk)
-            raw = ring.tile([P, 2, PACK * QUARTER], BF16, name="raw_heads", tag="ring")
-            for s in range(2):
-                cols = slice(s * HALF, (s + 1) * HALF)
-                nc.sync.dma_start(out=x_conv_rows[:, cols], in_=x_conv[:, cols])
-                nc.sync.dma_start(
-                    out=raw[:, s, :],
-                    in_=wk_w.rearrange("h (p j) o -> p h (j o)", j=PACK)[:, s, :],
-                )
-                raw_pieces[("k", s, s)] = raw[:, s, :].rearrange("p (j o) -> p j o", j=PACK)
-
         x_conv_rows = keep.tile([P, WIDTH], BF16, name="x_conv_rows")
         x_left_rows = keep.tile([P, WIDTH], BF16, name="x_left_rows")
         m_old = keep.tile([P, WIDTH], BF16, name="m_old")
         nc_old = keep.tile([P, 2, WIDTH], BF16, name="nc_old")
         bias_rows = keep.tile([P, P], BF16, name="bias_rows")
         nc.gpsimd.memset(bias_rows[96:P, :], 0.0)
-        load_first_chunk_and_x_conv()
+
+        def load_half_of_x_conv(half):
+            nc.sync.dma_start(
+                out=x_conv_rows[:, half_columns(half)], in_=x_conv[:, half_columns(half)]
+            )
+
+        load_next_chunk(load_half_of_x_conv)
         for r, matrix in enumerate(bias_order):
             nc.sync.dma_start(
                 out=bias_rows[r * BIAS_ROWS : (r + 1) * BIAS_ROWS, :],
@@ -148,7 +149,7 @@ def tile_mlstmblock_pb_kernel(
             )
         load_next_chunk()
         nc.sync.dma_start(out=x_left_rows[:], in_=x_left)
-        for other_more in range(RING - 2):
+        for more in range(RING - 2):
             load_next_chunk()
         nc.sync.dma_start(out=m_old[:], in_=m_prev)
         nc.sync.dma_start(out=nc_old[:, 0, :], in_=n_prev)
@@ -185,53 +186,76 @@ def tile_mlstmblock_pb_kernel(
                 out=codes[:, batch].bitcast(FP8X4), scales=scales[:, batch], in_=grouped[:]
             )
 
-        grouped_pieces = {}
-        quantised_pieces = {}
+        grouped_units = {}
+        quantised_units = {}
         banks = {}
-        def regroup(n):
-            piece, where = pieces[n]
-            grouped = work.tile(
-                [P, QUARTER, PACK], BF16, align_bytes=64, name="grouped", bufs=LEAD + 3
-            )
-            copy = nc.vector.tensor_copy if where == "vector" else nc.scalar.copy
-            copy(
-                out=grouped[:].rearrange("p (c i) j -> p c j i", i=RUN),
-                in_=raw_pieces[piece].rearrange("p j (c i) -> p c j i", i=RUN),
-            )
-            grouped_pieces[n] = grouped
-            if last_use[chunk_of(piece)] == n:
-                load_next_chunk()
+
+        def regroup(n, vector_part):
+            if n >= len(units):
+                return
+            unit, flags = units[n]
+            if n not in grouped_units:
+                grouped = work.tile(
+                    [P, HALF, PACK], BF16, align_bytes=64, name="grouped", bufs=GROUPED
+                )
+                grouped_units[n] = grouped
+            for s, piece in enumerate(unit):
+                if flags[s] != vector_part:
+                    continue
+                out = grouped_units[n][:, columns(s), :].rearrange("p (c i) j -> p c j i", i=RUN)
+                in_ = raw_pieces[piece].rearrange("p j (c i) -> p c j i", i=RUN)
+                if piece[0] == "i" and vector_part:
+                    nc.vector.tensor_scalar(
+                        out=out, in0=in_, scalar1=-1.0, scalar2=None, op0=ALU.mult
+                    )
+                elif piece[0] == "i":
+                    nc.scalar.activation(out=out, in_=in_, func=ACT.Copy, scale=-1.0)
+                elif vector_part:
+                    nc.vector.tensor_copy(out=out, in_=in_)
+                else:
+                    nc.scalar.copy(out=out, in_=in_)
+                left[chunk_of(piece)] -= 1
+                if left[chunk_of(piece)] == 0:
+                    load_next_chunk()
 
         def quantise(n):
-            codes = work.tile([P, QUARTER], U32, align_bytes=64, name="codes")
-            scales = work.tile([P, QUARTER], U8, align_bytes=64, name="scales")
+            width = len(units[n][0]) * QUARTER
+            codes = work.tile([P, HALF], U32, align_bytes=64, name="codes", bufs=3)
+            scales = work.tile([P, HALF], U8, align_bytes=64, name="scales", bufs=3)
             nc.vector.quantize_mx(
-                out=codes[:].bitcast(FP8X4),
-                scales=scales[:],
-                in_=grouped_pieces[n][:].rearrange("p w j -> p (w j)"),
+                out=codes[:, 0:width].bitcast(FP8X4),
+                scales=scales[:, 0:width],
+                in_=grouped_units[n][:, 0:width, :].rearrange("p w j -> p (w j)"),
             )
-            quantised_pieces[n] = (codes, scales)
+            quantised_units[n] = (codes, scales)
 
         def multiply(n):
-            (matrix, k_pass, quarter), other_where = pieces[n]
-            lone = matrix in "kvq"
-            if lone or k_pass == 0:
-                bank = psum.tile([P, QUARTER], F32, name="bank", tag="bank")
-                banks[(matrix, quarter)] = bank
-            codes, scales = quantised_pieces[n]
-            x_codes, x_scales = x_operands["left" if matrix in "vo" else "conv"]
-            batch = slice(k_pass * P, (k_pass + 1) * P)
-            nc.tensor.matmul_mx(
-                out=banks[(matrix, quarter)][:],
-                lhsT=x_codes[:, batch].bitcast(FP8X4),
-                lhsT_scale=x_scales[:, batch],
-                rhs=codes[:].bitcast(FP8X4),
-                rhs_scale=scales[:],
-                start=lone or k_pass == 0,
-                stop=lone or k_pass == K_PASSES - 1,
-            )
+            codes, scales = quantised_units[n]
+            for s, (matrix, k_pass, quarter) in enumerate(units[n][0]):
+                x_codes, x_scales = x_operands["left" if matrix in "vo" else "conv"]
+                batch = slice(k_pass * P, (k_pass + 1) * P)
+                first, last = k_pass == 0, k_pass == K_PASSES - 1
+                targets = {
+                    "i": [("i", first, last), ("d", first, False)],
+                    "f": [("d", False, last)],
+                    "o": [("o", first, last)],
+                }.get(matrix, [(matrix, True, True)])
+                for name, start, stop in targets:
+                    if start:
+                        bank = psum.tile([P, QUARTER], F32, name="bank", tag="bank")
+                        banks[(name, quarter)] = bank
+                    nc.tensor.matmul_mx(
+                        out=banks[(name, quarter)][:],
+                        lhsT=x_codes[:, batch].bitcast(FP8X4),
+                        lhsT_scale=x_scales[:, batch],
+                        rhs=codes[:, columns(s)].bitcast(FP8X4),
+                        rhs_scale=scales[:, columns(s)],
+                        start=start,
+                        stop=stop,
+                    )
 
         bias_turned = keep.tile([P, P], BF16, name="bias_turned")
+        difference = keep.tile([P, BIAS_ROWS], F32, name="difference")
         bias = {}
         bias_banks = {}
 
@@ -246,6 +270,17 @@ def tile_mlstmblock_pb_kernel(
                 )
             bias_banks[(matrix, half)] = spread
 
+        def spread_difference(s):
+            spread = psum.tile([P, QUARTER], F32, name="spread_difference", tag="bank")
+            for c in range(QUARTER // P):
+                column = s * (QUARTER // P) + c
+                nc.tensor.transpose(
+                    spread[:, c * P : (c + 1) * P],
+                    difference[:, column : column + 1].to_broadcast([P, P]),
+                    identity[:],
+                )
+            bias_banks[("f - i", s)] = spread
+
         def keep_bias(matrix, half):
             if half == 0:
                 kept = keep.tile([P, WIDTH], BF16, name="bias_" + matrix)
@@ -259,7 +294,7 @@ def tile_mlstmblock_pb_kernel(
         kv = keep.tile([P, 2, WIDTH], F32, name="kv")
         nc_new = keep.tile([P, 2, WIDTH], F32, name="nc_new")
         q = keep.tile([P, WIDTH], F32, name="q")
-        squares = keep.tile([P, QUARTERS], F32, name="squares")
+        squares = keep.tile([P, 2], F32, name="squares")
         norm = keep.tile([P, 1], F32, name="norm")
         half_over_denom = keep.tile([P, 1], F32, name="half_over_denom")
         temps = {}
@@ -271,8 +306,13 @@ def tile_mlstmblock_pb_kernel(
                 run()
             scalar_queue.clear()
 
+        def flush_stores():
+            for target, source in store_queue:
+                nc.sync.dma_start(out=target, in_=source)
+            store_queue.clear()
+
         def both(row):
-            return row.unsqueeze(1).to_broadcast([P, 2, QUARTER])
+            return row.unsqueeze(1).to_broadcast([P, 2, HALF])
 
         def add_bias(out, matrix, quarter):
             nc.vector.tensor_tensor(
@@ -280,7 +320,7 @@ def tile_mlstmblock_pb_kernel(
                 op=ALU.add,
             )
 
-        def item_none(other_s):
+        def item_none(s):
             return
 
         def item_k(s):
@@ -292,172 +332,197 @@ def tile_mlstmblock_pb_kernel(
         def item_q(s):
             add_bias(q[:, columns(s)], "q", s)
 
-        def item_fm(half):
-            cols = slice(half * HALF, (half + 1) * HALF)
+        def item_fm(s):
             nc.vector.tensor_tensor(
-                out=gates[:, 1, cols], in0=bias_banks[("f", half)][:], in1=m_old[:, cols],
-                op=ALU.add,
+                out=gates[:, 1, columns(s)], in0=bias_banks[("f - i", s)][:],
+                in1=m_old[:, columns(s)], op=ALU.add,
             )
 
         def item_i(s):
-            add_bias(gates[:, 0, columns(s)], "i", s)
+            nc.vector.scalar_tensor_tensor(
+                out=gates[:, 0, columns(s)], in0=banks[("i", s)][:], scalar=-1.0,
+                in1=bias["i"][:, columns(s)], op0=ALU.mult, op1=ALU.add,
+            )
 
-        def item_f(s):
+        def item_d(s):
             nc.vector.tensor_tensor(
-                out=gates[:, 1, columns(s)], in0=banks[("f", s)][:], in1=gates[:, 1, columns(s)],
+                out=gates[:, 1, columns(s)], in0=banks[("d", s)][:], in1=gates[:, 1, columns(s)],
                 op=ALU.add,
             )
 
-        def item_max(s):
-            m_t = work.tile([P, QUARTER], F32, name="m_t")
-            temps[("m", s)] = m_t
-            nc.vector.tensor_tensor(
-                out=m_t[:], in0=gates[:, 0, columns(s)], in1=gates[:, 1, columns(s)], op=ALU.max
+        def item_max(half):
+            cols = half_columns(half)
+            m_t = work.tile([P, HALF], F32, name="m_t", bufs=2)
+            nc.vector.scalar_tensor_tensor(
+                out=m_t[:], in0=gates[:, 1, cols], scalar=0.0, in1=gates[:, 0, cols],
+                op0=ALU.max, op1=ALU.add,
             )
-            store_queue.append((out_3[:, columns(s)], m_t[:]))
+            store_queue.append((out_3[:, cols], m_t[:]))
 
-        def item_sub(s):
-            both_gates = gates[:, :, columns(s)]
-            nc.vector.tensor_tensor(
-                out=both_gates, in0=both_gates, in1=both(temps[("m", s)][:]), op=ALU.subtract
+        def item_clip(half):
+            cols = half_columns(half)
+            nc.vector.tensor_scalar(
+                out=gates[:, 0, cols], in0=gates[:, 1, cols], scalar1=0.0, scalar2=-1.0,
+                op0=ALU.max, op1=ALU.mult,
+            )
+            nc.vector.tensor_scalar(
+                out=gates[:, 1, cols], in0=gates[:, 1, cols], scalar1=0.0, scalar2=None,
+                op0=ALU.min,
             )
 
             def exponentials():
-                nc.scalar.activation(out=both_gates, in_=both_gates, func=ACT.Exp)
+                nc.scalar.activation(
+                    out=gates[:, :, cols], in_=gates[:, :, cols], func=ACT.Exp
+                )
 
             scalar_queue.append(exponentials)
 
-        def item_ik(s):
+        def item_ik(half):
             flush_scalar()
+            cols = half_columns(half)
             nc.vector.tensor_tensor(
-                out=kv[:, 0, columns(s)], in0=kv[:, 0, columns(s)], in1=gates[:, 0, columns(s)],
+                out=kv[:, 0, cols], in0=kv[:, 0, cols], in1=gates[:, 0, cols], op=ALU.mult
+            )
+
+        def item_ikv(half):
+            cols = half_columns(half)
+            nc.vector.tensor_tensor(
+                out=kv[:, 1, cols], in0=kv[:, 1, cols], in1=kv[:, 0, cols], op=ALU.mult
+            )
+
+        def item_fnc(half):
+            flush_scalar()
+            cols = half_columns(half)
+            nc.vector.tensor_tensor(
+                out=nc_new[:, :, cols], in0=nc_old[:, :, cols], in1=both(gates[:, 1, cols]),
                 op=ALU.mult,
             )
 
-        def item_ikv(s):
-            nc.vector.tensor_tensor(
-                out=kv[:, 1, columns(s)], in0=kv[:, 1, columns(s)], in1=kv[:, 0, columns(s)],
-                op=ALU.mult,
-            )
-
-        def item_fnc(s):
-            flush_scalar()
-            nc.vector.tensor_tensor(
-                out=nc_new[:, :, columns(s)], in0=nc_old[:, :, columns(s)],
-                in1=both(gates[:, 1, columns(s)]), op=ALU.mult,
-            )
-
-        def item_nc(s):
+        def item_nc(half):
+            cols = half_columns(half)
             nc.vector.scalar_tensor_tensor(
-                out=nc_new[:, :, columns(s)], in0=kv[:, :, columns(s)], scalar=K_SCALE,
-                in1=nc_new[:, :, columns(s)], op0=ALU.mult, op1=ALU.add,
+                out=nc_new[:, :, cols], in0=kv[:, :, cols], scalar=K_SCALE,
+                in1=nc_new[:, :, cols], op0=ALU.mult, op1=ALU.add,
             )
-            store_queue.append((out_2[:, columns(s)], nc_new[:, 0, columns(s)]))
-            store_queue.append((out_1[:, columns(s)], nc_new[:, 1, columns(s)]))
+            store_queue.append((out_2[:, cols], nc_new[:, 0, cols]))
+            store_queue.append((out_1[:, cols], nc_new[:, 1, cols]))
 
-        def item_nq(s):
-            nq = work.tile([P, QUARTER], F32, name="nq", bufs=2)
+        def item_nq(half):
+            cols = half_columns(half)
+            nq = work.tile([P, HALF], F32, name="nq", bufs=1)
             nc.vector.tensor_tensor(
-                out=nq[:], in0=nc_new[:, 0, columns(s)], in1=q[:, columns(s)], op=ALU.mult
+                out=nq[:], in0=nc_new[:, 0, cols], in1=q[:, cols], op=ALU.mult
             )
 
             def square():
                 nc.scalar.activation(
-                    out=nq[:], in_=nq[:], func=ACT.Square, accum_out=squares[:, s : s + 1]
+                    out=nq[:], in_=nq[:], func=ACT.Square, accum_out=squares[:, half : half + 1]
                 )
 
             scalar_queue.append(square)
 
-        def item_sum(other_s):
+        def item_sum(s):
             flush_scalar()
             nc.vector.reduce_sum(out=norm[:], in_=squares[:], axis=mybir.AxisListType.X)
             nc.gpsimd.tensor_tensor(out=norm[:], in0=norm[:], in1=one_half[:], op=ALU.pow)
 
-        def item_denom(other_s):
+        def item_denom(s):
             nc.vector.tensor_scalar(
                 out=norm[:], in0=norm[:], scalar1=2.0, scalar2=2.0 * EPSILON,
                 op0=ALU.mult, op1=ALU.add,
             )
 
-        def item_reciprocal(other_s):
+        def item_reciprocal(s):
             nc.vector.reciprocal(out=half_over_denom[:], in_=norm[:])
 
-        def item_cq(s):
+        def item_cq(half):
+            cols = half_columns(half)
             nc.vector.scalar_tensor_tensor(
-                out=q[:, columns(s)], in0=nc_new[:, 1, columns(s)],
-                scalar=half_over_denom[:, 0:1], in1=q[:, columns(s)], op0=ALU.mult, op1=ALU.mult,
+                out=q[:, cols], in0=nc_new[:, 1, cols], scalar=half_over_denom[:, 0:1],
+                in1=q[:, cols], op0=ALU.mult, op1=ALU.mult,
             )
 
+        def output_parts(s):
+            parts = 2 if s == QUARTERS - 1 else 1
+            size = QUARTER // parts
+            return [
+                (slice(n * size, (n + 1) * size),
+                 slice(s * QUARTER + n * size, s * QUARTER + (n + 1) * size))
+                for n in range(parts)
+            ]
+
         def item_o(s):
+            flush_scalar()
             h_t = work.tile([P, QUARTER], F32, name="h_t")
-            temps[("h", s)] = h_t
-            add_bias(h_t[:], "o", s)
+            temps[s] = h_t
+            for part, wide in output_parts(s):
+                nc.vector.tensor_tensor(
+                    out=h_t[:, part], in0=banks[("o", s)][:, part], in1=bias["o"][:, wide],
+                    op=ALU.add,
+                )
 
             def tanh():
-                nc.scalar.activation(out=h_t[:], in_=h_t[:], func=ACT.Tanh, scale=0.5)
+                for part, wide in output_parts(s):
+                    nc.scalar.activation(
+                        out=h_t[:, part], in_=h_t[:, part], func=ACT.Tanh, scale=0.5
+                    )
 
             scalar_queue.append(tanh)
 
         def item_h(s):
             flush_scalar()
-            h_t = temps[("h", s)]
-            nc.vector.scalar_tensor_tensor(
-                out=h_t[:], in0=h_t[:], scalar=1.0, in1=q[:, columns(s)],
-                op0=ALU.add, op1=ALU.mult,
-            )
-            store_queue.append((out_0[:, columns(s)], h_t[:]))
+            h_t = temps[s]
+            for part, wide in output_parts(s):
+                nc.vector.scalar_tensor_tensor(
+                    out=h_t[:, part], in0=h_t[:, part], scalar=1.0, in1=q[:, wide],
+                    op0=ALU.add, op1=ALU.mult,
+                )
+                store_queue.append((out_0[:, wide], h_t[:, part]))
 
-        def update(a, b):
+        def update(half, between):
             return [
-                (1, item_f, a), (1, item_f, b), (1, item_max, a), (1, item_max, b),
-                (2, item_sub, a), (2, item_sub, b), (2, item_fnc, a), (1, item_ik, a),
-                (2, item_fnc, b), (1, item_ik, b), (1, item_ikv, a), (1, item_ikv, b),
-                (2, item_nc, a), (2, item_nc, b), (1, item_nq, a), (1, item_nq, b),
+                (1, item_d, 2 * half), (1, item_d, 2 * half + 1), (2, item_max, half),
+                (2, item_clip, half), *between, (2, item_ik, half), (4, item_fnc, half),
+                (2, item_ikv, half), (4, item_nc, half),
             ]
 
-        first_update = update(0, 1) + [(1, item_i, 2), (1, item_i, 3)]
-        last_update = update(2, 3) + [
-            (1, item_o, 0), (1, item_o, 1),
-            (1, item_sum, 0), (1, item_denom, 0), (1, item_reciprocal, 0),
-            (1, item_cq, 0), (1, item_cq, 1), (1, item_cq, 2), (1, item_cq, 3),
-            (1, item_o, 2), (1, item_h, 0), (1, item_h, 1),
-        ]
         carried = [
-            (0, 1, 0, [(2, item_none, 0)] + [(1, item_k, s) for s in range(4)] + [(1, item_v, s) for s in range(4)]
-                + [(1, item_q, s) for s in range(2)]),
-            (1, 1, 0, [(1, item_q, 2), (1, item_q, 3), (2, item_fm, 0), (2, item_fm, 1)]),
-            (2, 1, 0, [(1, item_i, 0), (1, item_i, 1)]),
-            (3, 2, 0, first_update),
-            (5, 2, 2, last_update),
+            (0, 1, 0, [(2, item_none, 0)] + [(1, item_k, s) for s in range(4)]
+                + [(1, item_v, s) for s in range(4)] + [(1, item_q, s) for s in range(2)]),
+            (1, 1, 0, [(1, item_q, 2), (1, item_q, 3), (2, item_none, 0)]),
+            (2, 1, 0, [(1, item_i, 0), (1, item_i, 1), (1, item_fm, 0), (1, item_fm, 1)]),
+            (3, 2, 0, update(0, [(1, item_fm, 2), (1, item_fm, 3)])
+                + [(1, item_i, 2), (1, item_i, 3)]),
+            (5, 2, 1, update(1, [(2, item_nq, 0)]) + [
+                (2, item_nq, 1), (1, item_o, 0), (1, item_o, 1),
+                (1, item_sum, 0), (1, item_denom, 0), (1, item_reciprocal, 0),
+                (2, item_cq, 0), (1, item_h, 0), (1, item_h, 1), (2, item_cq, 1),
+            ]),
         ]
         items_of_step = []
         for first, count, spare, items in carried:
             steps = sum(len(stages[first + n]) for n in range(count))
-            total = sum(units for units, other_item, other_s in items)
-            plan = [[] for other_step in range(steps)]
+            total = sum(size for size, item, s in items)
+            plan = [[] for step in range(steps)]
             offset = 0
-            for units, item, s in items:
-                step = min(steps - 1, (offset + units) * (steps - spare) // total)
+            for size, item, s in items:
+                step = min(steps - 1, (offset + size) * (steps - spare) // total)
                 plan[step].append((item, s))
-                offset += units
+                offset += size
             items_of_step.extend(plan)
-
-        def flush_stores():
-            for target, source in store_queue:
-                nc.sync.dma_start(out=target, in_=source)
-            store_queue.clear()
 
         for half in range(2):
             grouped_conv = turn_activations(x_conv_rows, "conv", half, nc.vector.tensor_copy)
             quantise_activations(grouped_conv, "conv", half)
         for n in range(LEAD):
-            regroup(n)
+            regroup(n, False)
+            regroup(n, True)
         bias_jobs = [(m, h) for m in ("k", "v", "q", "i", "o") for h in range(2)]
+        difference_steps = (12, 13, 16, 17)
 
-        for n in range(len(pieces)):
+        for n in range(len(units)):
             quantise(n)
-            if n + LEAD < len(pieces):
-                regroup(n + LEAD)
+            regroup(n + LEAD, False)
             if n == 0:
                 turned_bias = psum.tile([P, P], BF16, name="turned_bias", tag="bank")
                 nc.tensor.transpose(turned_bias[:], bias_rows[:], identity_bf16[:])
@@ -467,37 +532,33 @@ def tile_mlstmblock_pb_kernel(
                     turn_activations(x_left_rows, "left", half, nc.scalar.copy)
                     for half in range(2)
                 ]
-            if n == 3:
+            if n == 2:
                 for half in range(2):
                     quantise_activations(grouped_left[half], "left", half)
-            if n < len(bias_jobs):
-                spread_bias(*bias_jobs[n])
-            if n in (10, 11):
-                spread_bias("f", n - 10)
+            if n == 4:
+                f_first = list(bias_order).index("f") * BIAS_ROWS
+                i_first = list(bias_order).index("i") * BIAS_ROWS
+                nc.vector.tensor_tensor(
+                    out=difference[:], in0=bias_turned[:, f_first : f_first + BIAS_ROWS],
+                    in1=bias_turned[:, i_first : i_first + BIAS_ROWS], op=ALU.subtract,
+                )
+            for job in bias_jobs[2 * n : 2 * n + 2]:
+                spread_bias(*job)
+            if n in difference_steps:
+                spread_difference(difference_steps.index(n))
             multiply(n)
             flush_scalar()
-            if n < len(bias_jobs):
-                keep_bias(*bias_jobs[n])
+            for job in bias_jobs[2 * n : 2 * n + 2]:
+                keep_bias(*job)
             flush_stores()
-            for item, s in items_of_step[n]:
+            middle = (len(items_of_step[n]) + 1) // 2
+            for item, s in items_of_step[n][:middle]:
                 item(s)
-        flush_scalar()
-        h_t = work.tile([P, QUARTER], F32, name="h_t")
-        for part in range(2):
-            cols = slice(part * QUARTER // 2, (part + 1) * QUARTER // 2)
-            wide = slice(3 * QUARTER + cols.start, 3 * QUARTER + cols.stop)
-            nc.vector.tensor_tensor(
-                out=h_t[:, cols], in0=banks[("o", 3)][:, cols], in1=bias["o"][:, wide],
-                op=ALU.add,
-            )
-            nc.scalar.activation(out=h_t[:, cols], in_=h_t[:, cols], func=ACT.Tanh, scale=0.5)
+            regroup(n + LEAD, True)
+            for item, s in items_of_step[n][middle:]:
+                item(s)
+        item_o(2)
+        item_o(3)
         item_h(2)
+        item_h(3)
         flush_stores()
-        for part in range(2):
-            cols = slice(part * QUARTER // 2, (part + 1) * QUARTER // 2)
-            wide = slice(3 * QUARTER + cols.start, 3 * QUARTER + cols.stop)
-            nc.vector.scalar_tensor_tensor(
-                out=h_t[:, cols], in0=h_t[:, cols], scalar=1.0, in1=q[:, wide],
-                op0=ALU.add, op1=ALU.mult,
-            )
-            nc.sync.dma_start(out=out_0[:, wide], in_=h_t[:, cols])

@@ -142,6 +142,7 @@ def tile_mlstmblock_pb_kernel(
             )
 
         load_next_chunk(load_half_of_x_conv)
+        load_next_chunk()
         for r, matrix in enumerate(bias_order):
             nc.sync.dma_start(
                 out=bias_rows[r * BIAS_ROWS : (r + 1) * BIAS_ROWS, :],
@@ -149,11 +150,8 @@ def tile_mlstmblock_pb_kernel(
             )
         load_next_chunk()
         nc.sync.dma_start(out=x_left_rows[:], in_=x_left)
-        for more in range(RING - 2):
+        for more in range(RING - 3):
             load_next_chunk()
-        nc.sync.dma_start(out=m_old[:], in_=m_prev)
-        nc.sync.dma_start(out=nc_old[:, 0, :], in_=n_prev)
-        nc.sync.dma_start(out=nc_old[:, 1, :], in_=c_prev)
 
         identity_bf16 = keep.tile([P, P], BF16, name="identity_bf16")
         nc.vector.tensor_copy(out=identity_bf16[:], in_=identity[:])
@@ -522,6 +520,11 @@ def tile_mlstmblock_pb_kernel(
 
         for n in range(len(units)):
             quantise(n)
+            if n == 8:
+                nc.sync.dma_start(out=m_old[:], in_=m_prev)
+            if n == 12:
+                nc.sync.dma_start(out=nc_old[:, 0, :], in_=n_prev)
+                nc.sync.dma_start(out=nc_old[:, 1, :], in_=c_prev)
             regroup(n + LEAD, False)
             if n == 0:
                 turned_bias = psum.tile([P, P], BF16, name="turned_bias", tag="bank")

@@ -50,7 +50,7 @@ def tile_mlstmblock_pb_kernel(
 ):
     nc = tc.nc
     weights = {"k": wk_w, "v": wv_w, "q": wq_w, "i": wi_w, "f": wf_w, "o": wo_w}
-    bias_order = {"k": wk_b, "v": wv_b, "q": wq_b, "f": wf_b, "i": wi_b, "o": wo_b}
+    biases = {"k": wk_b, "v": wv_b, "q": wq_b, "i": wi_b, "o": wo_b}
 
     with ExitStack() as ctx:
         keep = ctx.enter_context(tc.tile_pool(name="keep", bufs=1))
@@ -73,7 +73,7 @@ def tile_mlstmblock_pb_kernel(
         stages[0][0:1] = [[piece] for piece in stages[0][0]]
         stages[-1][-1:] = [[piece] for piece in stages[-1][-1]]
 
-        on_vector_counts = [6, 4, 4, 3, 3, 2, 0]
+        on_vector_counts = [6, 4, 4, 4, 3, 2, 0]
         units = []
         for stage, share in zip(stages, on_vector_counts):
             count = sum(len(unit) for unit in stage)
@@ -134,7 +134,9 @@ def tile_mlstmblock_pb_kernel(
         m_old = keep.tile([P, WIDTH], BF16, name="m_old")
         nc_old = keep.tile([P, 2, WIDTH], BF16, name="nc_old")
         bias_rows = keep.tile([P, P], BF16, name="bias_rows")
-        nc.gpsimd.memset(bias_rows[96:P, :], 0.0)
+        nc.gpsimd.memset(bias_rows[:], 0.0)
+        gate_bias_rows = keep.tile([P, WIDTH], BF16, name="gate_bias_rows")
+        nc.gpsimd.memset(gate_bias_rows[:], 0.0)
 
         def load_half_of_x_conv(half):
             nc.sync.dma_start(
@@ -143,10 +145,10 @@ def tile_mlstmblock_pb_kernel(
 
         load_next_chunk(load_half_of_x_conv)
         load_next_chunk()
-        for r, matrix in enumerate(bias_order):
+        for r, matrix in enumerate("kvq"):
             nc.sync.dma_start(
                 out=bias_rows[r * BIAS_ROWS : (r + 1) * BIAS_ROWS, :],
-                in_=bias_order[matrix].rearrange("(c n) -> c n", n=P),
+                in_=biases[matrix].rearrange("(c n) -> c n", n=P),
             )
         load_next_chunk()
         nc.sync.dma_start(out=x_left_rows[:], in_=x_left)
@@ -155,6 +157,10 @@ def tile_mlstmblock_pb_kernel(
 
         identity_bf16 = keep.tile([P, P], BF16, name="identity_bf16")
         nc.vector.tensor_copy(out=identity_bf16[:], in_=identity[:])
+        plus_minus = keep.tile([P, 1], BF16, name="plus_minus")
+        nc.vector.tensor_tensor(
+            out=plus_minus[:], in0=identity[:, 0:1], in1=identity[:, 1:2], op=ALU.subtract
+        )
 
         x_operands = {}
 
@@ -253,12 +259,11 @@ def tile_mlstmblock_pb_kernel(
                     )
 
         bias_turned = keep.tile([P, P], BF16, name="bias_turned")
-        difference = keep.tile([P, BIAS_ROWS], F32, name="difference")
         bias = {}
         bias_banks = {}
 
         def spread_bias(matrix, half):
-            first = list(bias_order).index(matrix) * BIAS_ROWS + half * BIAS_ROWS // 2
+            first = "kvq".index(matrix) * BIAS_ROWS + half * BIAS_ROWS // 2
             spread = psum.tile([P, HALF], BF16, name="spread", tag="bank")
             for c in range(HALF // P):
                 nc.tensor.transpose(
@@ -268,16 +273,29 @@ def tile_mlstmblock_pb_kernel(
                 )
             bias_banks[(matrix, half)] = spread
 
-        def spread_difference(s):
-            spread = psum.tile([P, QUARTER], F32, name="spread_difference", tag="bank")
-            for c in range(QUARTER // P):
-                column = s * (QUARTER // P) + c
-                nc.tensor.transpose(
-                    spread[:, c * P : (c + 1) * P],
-                    difference[:, column : column + 1].to_broadcast([P, P]),
-                    identity[:],
-                )
-            bias_banks[("f - i", s)] = spread
+        shifts = []
+
+        def shift_gate(s):
+            shift = psum.tile([P, QUARTER], F32, name="shift", tag="bank")
+            nc.tensor.matmul(
+                out=shift[:], lhsT=identity_bf16[:], rhs=m_old[:, columns(s)],
+                start=True, stop=False,
+            )
+            nc.tensor.matmul(
+                out=shift[:], lhsT=plus_minus[:].to_broadcast([P, P]),
+                rhs=gate_bias_rows[:, columns(s)], start=False, stop=True,
+            )
+            shifts.append((s, shift))
+
+        def keep_shift():
+            for s, shift in shifts:
+                nc.scalar.copy(out=gates[:, 1, columns(s)], in_=shift[:])
+            shifts.clear()
+
+        def load_bias(matrix):
+            kept = keep.tile([P, WIDTH], BF16, name="bias_" + matrix)
+            bias[matrix] = kept
+            nc.sync.dma_start(out=kept[:], in_=biases[matrix].partition_broadcast(P))
 
         def keep_bias(matrix, half):
             if half == 0:
@@ -329,12 +347,6 @@ def tile_mlstmblock_pb_kernel(
 
         def item_q(s):
             add_bias(q[:, columns(s)], "q", s)
-
-        def item_fm(s):
-            nc.vector.tensor_tensor(
-                out=gates[:, 1, columns(s)], in0=bias_banks[("f - i", s)][:],
-                in1=m_old[:, columns(s)], op=ALU.add,
-            )
 
         def item_i(s):
             nc.vector.scalar_tensor_tensor(
@@ -488,8 +500,8 @@ def tile_mlstmblock_pb_kernel(
             (0, 1, 0, [(2, item_none, 0)] + [(1, item_k, s) for s in range(4)]
                 + [(1, item_v, s) for s in range(4)] + [(1, item_q, s) for s in range(2)]),
             (1, 1, 0, [(1, item_q, 2), (1, item_q, 3), (2, item_none, 0)]),
-            (2, 1, 0, [(1, item_i, 0), (1, item_i, 1), (1, item_fm, 0), (1, item_fm, 1)]),
-            (3, 2, 0, update(0, [(1, item_fm, 2), (1, item_fm, 3)])
+            (2, 1, 0, [(1, item_i, 0), (1, item_i, 1)]),
+            (3, 2, 0, update(0, [(4, item_none, 0)])
                 + [(1, item_i, 2), (1, item_i, 3)]),
             (5, 2, 1, update(1, [(2, item_nq, 0)]) + [
                 (2, item_nq, 1), (1, item_o, 0), (1, item_o, 1),
@@ -515,16 +527,23 @@ def tile_mlstmblock_pb_kernel(
         for n in range(LEAD):
             regroup(n, False)
             regroup(n, True)
-        bias_jobs = [(m, h) for m in ("k", "v", "q", "i", "o") for h in range(2)]
-        difference_steps = (12, 13, 16, 17)
+        bias_jobs = [(m, h) for m in ("k", "v", "q") for h in range(2)]
+        shift_steps = (10, 11, 14, 15)
 
+        late_biases = {3: "i", 14: "o"}
         for n in range(len(units)):
             quantise(n)
-            if n == 8:
+            if n + 1 in shift_steps:
+                shift_gate(shift_steps.index(n + 1))
+            if n == 4:
                 nc.sync.dma_start(out=m_old[:], in_=m_prev)
+                nc.sync.dma_start(out=gate_bias_rows[0:1, :], in_=wf_b.unsqueeze(0))
+                nc.sync.dma_start(out=gate_bias_rows[1:2, :], in_=wi_b.unsqueeze(0))
             if n == 12:
                 nc.sync.dma_start(out=nc_old[:, 0, :], in_=n_prev)
                 nc.sync.dma_start(out=nc_old[:, 1, :], in_=c_prev)
+            if n in late_biases:
+                load_bias(late_biases[n])
             regroup(n + LEAD, False)
             if n == 0:
                 turned_bias = psum.tile([P, P], BF16, name="turned_bias", tag="bank")
@@ -535,22 +554,14 @@ def tile_mlstmblock_pb_kernel(
                     turn_activations(x_left_rows, "left", half, nc.scalar.copy)
                     for half in range(2)
                 ]
-            if n == 2:
+            if n == 3:
                 for half in range(2):
                     quantise_activations(grouped_left[half], "left", half)
-            if n == 4:
-                f_first = list(bias_order).index("f") * BIAS_ROWS
-                i_first = list(bias_order).index("i") * BIAS_ROWS
-                nc.vector.tensor_tensor(
-                    out=difference[:], in0=bias_turned[:, f_first : f_first + BIAS_ROWS],
-                    in1=bias_turned[:, i_first : i_first + BIAS_ROWS], op=ALU.subtract,
-                )
             for job in bias_jobs[2 * n : 2 * n + 2]:
                 spread_bias(*job)
-            if n in difference_steps:
-                spread_difference(difference_steps.index(n))
             multiply(n)
             flush_scalar()
+            keep_shift()
             for job in bias_jobs[2 * n : 2 * n + 2]:
                 keep_bias(*job)
             flush_stores()

from contextlib import ExitStack
import math

import concourse.mybir as mybir
from concourse.masks import make_identity

BF16 = mybir.dt.bfloat16
F32 = mybir.dt.float32
U32 = mybir.dt.uint32
U8 = mybir.dt.uint8
FP8X4 = mybir.dt.float8_e4m3fn_x4
ALU = mybir.AluOpType
ACT = mybir.ActivationFunctionType

P = 128
PACK = 4
K_PASS = P * PACK
WIDTH = 2048
QUARTER = 512
QUARTERS = WIDTH // QUARTER
HALF = 2 * QUARTER
K_PASSES = WIDTH // K_PASS
BIAS_ROWS = WIDTH // P

RUN = 2
RING = 7
LEAD = 2
GROUPED = 4
PSUM_BANKS = 8

K_SCALE = 1.0 / math.sqrt(QUARTER)
EPSILON = 1e-6

FLOPS = 2 * P * (3 * WIDTH * WIDTH + 3 * QUARTERS * QUARTER * QUARTER)


def half_columns(half):
    return slice(half * HALF, (half + 1) * HALF)


def columns(quarter):
    return slice(quarter * QUARTER, (quarter + 1) * QUARTER)


def tile_mlstmblock_pb_kernel(
    tc,
    x_conv, x_left, c_prev, n_prev, m_prev,
    wq_w, wq_b, wk_w, wk_b, wv_w, wv_b, wi_w, wi_b, wf_w, wf_b, wo_w, wo_b,
    out_0, out_1, out_2, out_3,
):
    nc = tc.nc
    weights = {"k": wk_w, "v": wv_w, "q": wq_w, "i": wi_w, "f": wf_w, "o": wo_w}
    biases = {"k": wk_b, "v": wv_b, "q": wq_b, "i": wi_b, "o": wo_b}

    with ExitStack() as ctx:
        keep = ctx.enter_context(tc.tile_pool(name="keep", bufs=1))
        ring = ctx.enter_context(tc.tile_pool(name="ring", bufs=RING))
        work = ctx.enter_context(tc.tile_pool(name="work", bufs=4))
        psum = ctx.enter_context(tc.psum_pool(name="psum", bufs=PSUM_BANKS))

        identity = keep.tile([P, P], F32, name="identity")
        make_identity(nc, identity[:])
        ctx.enter_context(tc.manual_schedule())

        def pair(matrix, k_pass, half):
            if matrix in "kvq":
                return [(matrix, 2 * half + s, 2 * half + s) for s in range(2)]
            return [(matrix, k_pass, 2 * half + s) for s in range(2)]

        stages = [[pair(matrix, None, half) for matrix in "kvq" for half in range(2)]]
        for matrix, half in (("i", 0), ("f", 0), ("i", 1), ("f", 1), ("o", 0), ("o", 1)):
            stages.append([pair(matrix, k_pass, half) for k_pass in range(K_PASSES)])
        stages[0][0:1] = [[piece] for piece in stages[0][0]]
        stages[-1][-1:] = [[piece] for piece in stages[-1][-1]]

        on_vector_counts = [6, 4, 4, 4, 3, 2, 0]
        units = []
        for stage, share in zip(stages, on_vector_counts):
            count = sum(len(unit) for unit in stage)
            t = 0
            for unit in stage:
                flags = []
                for piece in unit:
                    flags.append((t + 1) * share // count > t * share // count)
                    t += 1
                units.append((unit, flags))

        def chunk_of(piece):
            matrix, k_pass, quarter = piece
            return (matrix, None if matrix in "kvq" else k_pass, quarter // 2)

        chunk_order = []
        for unit, flags in units:
            if chunk_of(unit[0]) not in chunk_order:
                chunk_order.append(chunk_of(unit[0]))
        left = {chunk: 2 for chunk in chunk_order}

        raw_pieces = {}
        loaded = []

        def load_next_chunk(before_piece=None):
            if len(loaded) == len(chunk_order):
                return
            matrix, k_pass, half = chunk_order[len(loaded)]
            loaded.append(half)
            source = weights[matrix]
            if matrix in "kvq":
                raw = ring.tile([P, 2, PACK * QUARTER], BF16, name="raw_heads", tag="ring")
                for s in range(2):
                    head = 2 * half + s
                    if before_piece is not None:
                        before_piece(s)
                    nc.sync.dma_start(
                        out=raw[:, s, :],
                        in_=source.rearrange("h (p j) o -> p h (j o)", j=PACK)[:, head, :],
                    )
                    raw_pieces[(matrix, head, head)] = raw[:, s, :].rearrange(
                        "p (j o) -> p j o", j=PACK
                    )
            else:
                raw = ring.tile([P, PACK, HALF], BF16, name="raw_dense", tag="ring")
                rows = source[k_pass * K_PASS : (k_pass + 1) * K_PASS, half_columns(half)]
                nc.sync.dma_start(out=raw[:], in_=rows.rearrange("(p j) n -> p j n", j=PACK))
                for s in range(2):
                    raw_pieces[(matrix, k_pass, 2 * half + s)] = raw[:, :, columns(s)]

        one_half = keep.tile([P, 1], F32, name="one_half")
        warm = keep.tile([P, 1], F32, name="warm")
        nc.vector.memset(one_half[:], 0.5)
        nc.scalar.activation(out=warm[:], in_=one_half[:], func=ACT.Exp)

        x_conv_rows = keep.tile([P, WIDTH], BF16, name="x_conv_rows")
        x_left_rows = keep.tile([P, WIDTH], BF16, name="x_left_rows")
        m_old = keep.tile([P, WIDTH], BF16, name="m_old")
        nc_old = keep.tile([P, 2, WIDTH], BF16, name="nc_old")
        bias_rows = keep.tile([P, P], BF16, name="bias_rows")
        nc.gpsimd.memset(bias_rows[:], 0.0)
        gate_bias_rows = keep.tile([P, WIDTH], BF16, name="gate_bias_rows")
        nc.gpsimd.memset(gate_bias_rows[:], 0.0)

        def load_half_of_x_conv(half):
            nc.sync.dma_start(
                out=x_conv_rows[:, half_columns(half)], in_=x_conv[:, half_columns(half)]
            )

        load_next_chunk(load_half_of_x_conv)
        load_next_chunk()
        for r, matrix in enumerate("kvq"):
            nc.sync.dma_start(
                out=bias_rows[r * BIAS_ROWS : (r + 1) * BIAS_ROWS, :],
                in_=biases[matrix].rearrange("(c n) -> c n", n=P),
            )
        load_next_chunk()
        nc.sync.dma_start(out=x_left_rows[:], in_=x_left)
        for more in range(RING - 3):
            load_next_chunk()

        identity_bf16 = keep.tile([P, P], BF16, name="identity_bf16")
        nc.vector.tensor_copy(out=identity_bf16[:], in_=identity[:])
        plus_minus = keep.tile([P, 1], BF16, name="plus_minus")
        nc.vector.tensor_tensor(
            out=plus_minus[:], in0=identity[:, 0:1], in1=identity[:, 1:2], op=ALU.subtract
        )

        x_operands = {}

        def turn_activations(x_rows, name, half, copy_out):
            words = x_rows[:].bitcast(F32).rearrange("b (c p u) -> b c u p", p=P, u=2)
            grouped = work.tile([P, HALF], BF16, align_bytes=64, name="x_grouped", bufs=2)
            turned = psum.tile([P, 2, 2, P], F32, name="turned", tag="bank")
            for c in range(2):
                for u in range(2):
                    nc.tensor.transpose(
                        turned[:, c, u, :], words[:, 2 * half + c, u, :], identity[:]
                    )
            copy_out(
                out=grouped[:].bitcast(F32).rearrange("p (c b u) -> p c b u", b=P, u=2),
                in_=turned[:].rearrange("p c u b -> p c b u"),
            )
            if half == 0:
                codes = keep.tile([P, K_PASSES * P], U32, align_bytes=64, name=name + "_codes")
                scales = keep.tile([P, K_PASSES * P], U8, align_bytes=64, name=name + "_scales")
                x_operands[name] = (codes, scales)
            return grouped

        def quantise_activations(grouped, name, half):
            codes, scales = x_operands[name]
            batch = slice(half * 2 * P, (half + 1) * 2 * P)
            nc.vector.quantize_mx(
                out=codes[:, batch].bitcast(FP8X4), scales=scales[:, batch], in_=grouped[:]
            )

        grouped_units = {}
        quantised_units = {}
        banks = {}

        def regroup(n, vector_part):
            if n >= len(units):
                return
            unit, flags = units[n]
            if n not in grouped_units:
                grouped = work.tile(
                    [P, HALF, PACK], BF16, align_bytes=64, name="grouped", bufs=GROUPED
                )
                grouped_units[n] = grouped
            for s, piece in enumerate(unit):
                if flags[s] != vector_part:
                    continue
                out = grouped_units[n][:, columns(s), :].rearrange("p (c i) j -> p c j i", i=RUN)
                in_ = raw_pieces[piece].rearrange("p j (c i) -> p c j i", i=RUN)
                if piece[0] == "i" and vector_part:
                    nc.vector.tensor_scalar(
                        out=out, in0=in_, scalar1=-1.0, scalar2=None, op0=ALU.mult
                    )
                elif piece[0] == "i":
                    nc.scalar.activation(out=out, in_=in_, func=ACT.Copy, scale=-1.0)
                elif vector_part:
                    nc.vector.tensor_copy(out=out, in_=in_)
                else:
                    nc.scalar.copy(out=out, in_=in_)
                left[chunk_of(piece)] -= 1
                if left[chunk_of(piece)] == 0:
                    load_next_chunk()

        def quantise(n):
            width = len(units[n][0]) * QUARTER
            codes = work.tile([P, HALF], U32, align_bytes=64, name="codes", bufs=3)
            scales = work.tile([P, HALF], U8, align_bytes=64, name="scales", bufs=3)
            nc.vector.quantize_mx(
                out=codes[:, 0:width].bitcast(FP8X4),
                scales=scales[:, 0:width],
                in_=grouped_units[n][:, 0:width, :].rearrange("p w j -> p (w j)"),
            )
            quantised_units[n] = (codes, scales)

        def multiply(n):
            codes, scales = quantised_units[n]
            for s, (matrix, k_pass, quarter) in enumerate(units[n][0]):
                x_codes, x_scales = x_operands["left" if matrix in "vo" else "conv"]
                batch = slice(k_pass * P, (k_pass + 1) * P)
                first, last = k_pass == 0, k_pass == K_PASSES - 1
                targets = {
                    "i": [("i", first, last), ("d", first, False)],
                    "f": [("d", False, last)],
                    "o": [("o", first, last)],
                }.get(matrix, [(matrix, True, True)])
                for name, start, stop in targets:
                    if start:
                        bank = psum.tile([P, QUARTER], F32, name="bank", tag="bank")
                        banks[(name, quarter)] = bank
                    nc.tensor.matmul_mx(
                        out=banks[(name, quarter)][:],
                        lhsT=x_codes[:, batch].bitcast(FP8X4),
                        lhsT_scale=x_scales[:, batch],
                        rhs=codes[:, columns(s)].bitcast(FP8X4),
                        rhs_scale=scales[:, columns(s)],
                        start=start,
                        stop=stop,
                    )

        bias_turned = keep.tile([P, P], BF16, name="bias_turned")
        bias = {}
        bias_banks = {}

        def spread_bias(matrix, half):
            first = "kvq".index(matrix) * BIAS_ROWS + half * BIAS_ROWS // 2
            spread = psum.tile([P, HALF], BF16, name="spread", tag="bank")
            for c in range(HALF // P):
                nc.tensor.transpose(
                    spread[:, c * P : (c + 1) * P],
                    bias_turned[:, first + c : first + c + 1].to_broadcast([P, P]),
                    identity_bf16[:],
                )
            bias_banks[(matrix, half)] = spread

        shifts = []

        def shift_gate(s):
            shift = psum.tile([P, QUARTER], F32, name="shift", tag="bank")
            nc.tensor.matmul(
                out=shift[:], lhsT=identity_bf16[:], rhs=m_old[:, columns(s)],
                start=True, stop=False,
            )
            nc.tensor.matmul(
                out=shift[:], lhsT=plus_minus[:].to_broadcast([P, P]),
                rhs=gate_bias_rows[:, columns(s)], start=False, stop=True,
            )
            shifts.append((s, shift))

        def keep_shift():
            for s, shift in shifts:
                nc.scalar.copy(out=gates[:, 1, columns(s)], in_=shift[:])
            shifts.clear()

        def load_bias(matrix):
            kept = keep.tile([P, WIDTH], BF16, name="bias_" + matrix)
            bias[matrix] = kept
            nc.sync.dma_start(out=kept[:], in_=biases[matrix].partition_broadcast(P))

        def keep_bias(matrix, half):
            if half == 0:
                kept = keep.tile([P, WIDTH], BF16, name="bias_" + matrix)
                bias[matrix] = kept
            nc.scalar.copy(
                out=bias[matrix][:, half * HALF : (half + 1) * HALF],
                in_=bias_banks[(matrix, half)][:],
            )

        gates = keep.tile([P, 2, WIDTH], F32, name="gates")
        kv = keep.tile([P, 2, WIDTH], F32, name="kv")
        nc_new = keep.tile([P, 2, WIDTH], F32, name="nc_new")
        q = keep.tile([P, WIDTH], F32, name="q")
        squares = keep.tile([P, 2], F32, name="squares")
        norm = keep.tile([P, 1], F32, name="norm")
        half_over_denom = keep.tile([P, 1], F32, name="half_over_denom")
        temps = {}
        scalar_queue = []
        store_queue = []

        def flush_scalar():
            for run in scalar_queue:
                run()
            scalar_queue.clear()

        def flush_stores():
            for target, source in store_queue:
                nc.sync.dma_start(out=target, in_=source)
            store_queue.clear()

        def both(row):
            return row.unsqueeze(1).to_broadcast([P, 2, HALF])

        def add_bias(out, matrix, quarter):
            nc.vector.tensor_tensor(
                out=out, in0=banks[(matrix, quarter)][:], in1=bias[matrix][:, columns(quarter)],
                op=ALU.add,
            )

        def item_none(s):
            return

        def item_k(s):
            add_bias(kv[:, 0, columns(s)], "k", s)

        def item_v(s):
            add_bias(kv[:, 1, columns(s)], "v", s)

        def item_q(s):
            add_bias(q[:, columns(s)], "q", s)

        def item_i(s):
            nc.vector.scalar_tensor_tensor(
                out=gates[:, 0, columns(s)], in0=banks[("i", s)][:], scalar=-1.0,
                in1=bias["i"][:, columns(s)], op0=ALU.mult, op1=ALU.add,
            )

        def item_d(s):
            nc.vector.tensor_tensor(
                out=gates[:, 1, columns(s)], in0=banks[("d", s)][:], in1=gates[:, 1, columns(s)],
                op=ALU.add,
            )

        def item_max(half):
            cols = half_columns(half)
            m_t = work.tile([P, HALF], F32, name="m_t", bufs=2)
            nc.vector.scalar_tensor_tensor(
                out=m_t[:], in0=gates[:, 1, cols], scalar=0.0, in1=gates[:, 0, cols],
                op0=ALU.max, op1=ALU.add,
            )
            store_queue.append((out_3[:, cols], m_t[:]))

        def item_clip(half):
            cols = half_columns(half)
            nc.vector.tensor_scalar(
                out=gates[:, 0, cols], in0=gates[:, 1, cols], scalar1=0.0, scalar2=-1.0,
                op0=ALU.max, op1=ALU.mult,
            )
            nc.vector.tensor_scalar(
                out=gates[:, 1, cols], in0=gates[:, 1, cols], scalar1=0.0, scalar2=None,
                op0=ALU.min,
            )

            def exponentials():
                nc.scalar.activation(
                    out=gates[:, :, cols], in_=gates[:, :, cols], func=ACT.Exp
                )

            scalar_queue.append(exponentials)

        def item_ik(half):
            flush_scalar()
            cols = half_columns(half)
            nc.vector.tensor_tensor(
                out=kv[:, 0, cols], in0=kv[:, 0, cols], in1=gates[:, 0, cols], op=ALU.mult
            )

        def item_ikv(half):
            cols = half_columns(half)
            nc.vector.tensor_tensor(
                out=kv[:, 1, cols], in0=kv[:, 1, cols], in1=kv[:, 0, cols], op=ALU.mult
            )

        def item_fnc(half):
            flush_scalar()
            cols = half_columns(half)
            nc.vector.tensor_tensor(
                out=nc_new[:, :, cols], in0=nc_old[:, :, cols], in1=both(gates[:, 1, cols]),
                op=ALU.mult,
            )

        def item_nc(half):
            cols = half_columns(half)
            nc.vector.scalar_tensor_tensor(
                out=nc_new[:, :, cols], in0=kv[:, :, cols], scalar=K_SCALE,
                in1=nc_new[:, :, cols], op0=ALU.mult, op1=ALU.add,
            )
            store_queue.append((out_2[:, cols], nc_new[:, 0, cols]))
            store_queue.append((out_1[:, cols], nc_new[:, 1, cols]))

        def item_nq(half):
            cols = half_columns(half)
            nq = work.tile([P, HALF], F32, name="nq", bufs=1)
            nc.vector.tensor_tensor(
                out=nq[:], in0=nc_new[:, 0, cols], in1=q[:, cols], op=ALU.mult
            )

            def square():
                nc.scalar.activation(
                    out=nq[:], in_=nq[:], func=ACT.Square, accum_out=squares[:, half : half + 1]
                )

            scalar_queue.append(square)

        def item_sum(s):
            flush_scalar()
            nc.vector.reduce_sum(out=norm[:], in_=squares[:], axis=mybir.AxisListType.X)
            nc.gpsimd.tensor_tensor(out=norm[:], in0=norm[:], in1=one_half[:], op=ALU.pow)

        def item_denom(s):
            nc.vector.tensor_scalar(
                out=norm[:], in0=norm[:], scalar1=2.0, scalar2=2.0 * EPSILON,
                op0=ALU.mult, op1=ALU.add,
            )

        def item_reciprocal(s):
            nc.vector.reciprocal(out=half_over_denom[:], in_=norm[:])

        def item_cq(half):
            cols = half_columns(half)
            nc.vector.scalar_tensor_tensor(
                out=q[:, cols], in0=nc_new[:, 1, cols], scalar=half_over_denom[:, 0:1],
                in1=q[:, cols], op0=ALU.mult, op1=ALU.mult,
            )

        def output_parts(s):
            parts = 2 if s == QUARTERS - 1 else 1
            size = QUARTER // parts
            return [
                (slice(n * size, (n + 1) * size),
                 slice(s * QUARTER + n * size, s * QUARTER + (n + 1) * size))
                for n in range(parts)
            ]

        def item_o(s):
            flush_scalar()
            h_t = work.tile([P, QUARTER], F32, name="h_t")
            temps[s] = h_t
            for part, wide in output_parts(s):
                nc.vector.tensor_tensor(
                    out=h_t[:, part], in0=banks[("o", s)][:, part], in1=bias["o"][:, wide],
                    op=ALU.add,
                )

            def tanh():
                for part, wide in output_parts(s):
                    nc.scalar.activation(
                        out=h_t[:, part], in_=h_t[:, part], func=ACT.Tanh, scale=0.5
                    )

            scalar_queue.append(tanh)

        def item_h(s):
            flush_scalar()
            h_t = temps[s]
            for part, wide in output_parts(s):
                nc.vector.scalar_tensor_tensor(
                    out=h_t[:, part], in0=h_t[:, part], scalar=1.0, in1=q[:, wide],
                    op0=ALU.add, op1=ALU.mult,
                )
                store_queue.append((out_0[:, wide], h_t[:, part]))

        def update(half, between):
            return [
                (1, item_d, 2 * half), (1, item_d, 2 * half + 1), (2, item_max, half),
                (2, item_clip, half), *between, (2, item_ik, half), (4, item_fnc, half),
                (2, item_ikv, half), (4, item_nc, half),
            ]

        carried = [
            (0, 1, 0, [(2, item_none, 0)] + [(1, item_k, s) for s in range(4)]
                + [(1, item_v, s) for s in range(4)] + [(1, item_q, s) for s in range(2)]),
            (1, 1, 0, [(1, item_q, 2), (1, item_q, 3), (2, item_none, 0)]),
            (2, 1, 0, [(1, item_i, 0), (1, item_i, 1)]),
            (3, 2, 0, update(0, [(4, item_none, 0)])
                + [(1, item_i, 2), (1, item_i, 3)]),
            (5, 2, 1, update(1, [(2, item_nq, 0)]) + [
                (2, item_nq, 1), (1, item_o, 0), (1, item_o, 1),
                (1, item_sum, 0), (1, item_denom, 0), (1, item_reciprocal, 0),
                (2, item_cq, 0), (1, item_h, 0), (1, item_h, 1), (2, item_cq, 1),
            ]),
        ]
        items_of_step = []
        for first, count, spare, items in carried:
            steps = sum(len(stages[first + n]) for n in range(count))
            total = sum(size for size, item, s in items)
            plan = [[] for step in range(steps)]
            offset = 0
            for size, item, s in items:
                step = min(steps - 1, (offset + size) * (steps - spare) // total)
                plan[step].append((item, s))
                offset += size
            items_of_step.extend(plan)

        for half in range(2):
            grouped_conv = turn_activations(x_conv_rows, "conv", half, nc.vector.tensor_copy)
            quantise_activations(grouped_conv, "conv", half)
        for n in range(LEAD):
            regroup(n, False)
            regroup(n, True)
        bias_jobs = [(m, h) for m in ("k", "v", "q") for h in range(2)]
        shift_steps = (10, 11, 14, 15)

        late_biases = {3: "i", 14: "o"}
        for n in range(len(units)):
            quantise(n)
            if n + 1 in shift_steps:
                shift_gate(shift_steps.index(n + 1))
            if n == 4:
                nc.sync.dma_start(out=m_old[:], in_=m_prev)
                nc.sync.dma_start(out=gate_bias_rows[0:1, :], in_=wf_b.unsqueeze(0))
                nc.sync.dma_start(out=gate_bias_rows[1:2, :], in_=wi_b.unsqueeze(0))
            if n == 12:
                nc.sync.dma_start(out=nc_old[:, 0, :], in_=n_prev)
                nc.sync.dma_start(out=nc_old[:, 1, :], in_=c_prev)
            if n in late_biases:
                load_bias(late_biases[n])
            regroup(n + LEAD, False)
            if n == 0:
                turned_bias = psum.tile([P, P], BF16, name="turned_bias", tag="bank")
                nc.tensor.transpose(turned_bias[:], bias_rows[:], identity_bf16[:])
                nc.vector.tensor_copy(out=bias_turned[:], in_=turned_bias[:])
            if n == 1:
                grouped_left = [
                    turn_activations(x_left_rows, "left", half, nc.scalar.copy)
                    for half in range(2)
                ]
            if n == 3:
                for half in range(2):
                    quantise_activations(grouped_left[half], "left", half)
            for job in bias_jobs[2 * n : 2 * n + 2]:
                spread_bias(*job)
            multiply(n)
            flush_scalar()
            keep_shift()
            for job in bias_jobs[2 * n : 2 * n + 2]:
                keep_bias(*job)
            flush_stores()
            middle = (len(items_of_step[n]) + 1) // 2
            for item, s in items_of_step[n][:middle]:
                item(s)
            regroup(n + LEAD, True)
            for item, s in items_of_step[n][middle:]:
                item(s)
        item_o(2)
        item_o(3)
        item_h(2)
        item_h(3)
        flush_stores()
